import numpy as np
import ml_dtypes


def mxq(x, axis, fmt="e4m3"):
    dtype, down = {"e4m3": (ml_dtypes.float8_e4m3fn, 7), "e5m2": (ml_dtypes.float8_e5m2, 14)}[fmt]
    v = np.moveaxis(np.asarray(x, np.float32).astype(ml_dtypes.bfloat16).astype(np.float64), axis, -1)
    blocks = v.reshape(v.shape[:-1] + (-1, 32))
    amax = np.abs(blocks).max(-1, keepdims=True)
    byte = np.maximum(np.where(amax > 0, np.frexp(amax)[1] - 1 + 127, 0) - down, 1)
    scale = np.exp2(byte - 127.0)
    codes = (blocks / scale).astype(np.float32).astype(dtype).astype(np.float64)
    return np.moveaxis((codes * scale).reshape(v.shape), -1, axis)


WIDE = False


def mx_kscale(k):
    if not WIDE:
        return np.ones(k)
    levels = np.array([10, -10, 5, -5, 0])
    a = np.random.permutation(np.resize(levels, k // 512 * 4)).reshape(k // 512, 4)
    idx = np.arange(k)
    return np.exp2(a[idx // 512, idx % 128 // 32])


BF16 = ml_dtypes.bfloat16


def bf(x):
    return np.asarray(x, np.float32).astype(BF16)


def f64(x):
    return np.asarray(x).astype(np.float64)


E2M1 = np.array([0.0, 0.5, 1.0, 1.5, 2.0, 3.0, 4.0, 6.0, -0.0, -0.5, -1.0, -1.5, -2.0, -3.0, -4.0, -6.0])


def pack_weight(w, fmt):
    k, n = w.shape
    w = f64(bf(w)).reshape(k // 32, 32, n)
    amax = np.abs(w).max(1)
    if fmt == "e4m3":
        byte = np.frexp(amax)[1] - 1 + 127 - 7
    else:
        mant, ex = np.frexp(amax / 6.0)
        byte = np.where(mant > 0.5, ex, ex - 1) + 127
    byte = np.clip(np.where(amax > 0, byte, 1), 1, 254)
    scaled = (w * np.exp2(127.0 - byte)[:, None, :]).reshape(k, n).astype(np.float32)
    by_word = np.ascontiguousarray(scaled.reshape(k // 512, 128, 4, n).transpose(0, 1, 3, 2))
    if fmt == "e4m3":
        words = by_word.astype(ml_dtypes.float8_e4m3fn).view(np.uint8)
    else:
        c = by_word.astype(ml_dtypes.float4_e2m1fn).view(np.uint8) & 0xF
        words = c[..., 0::2] | (c[..., 1::2] << 4)
    return np.ascontiguousarray(words), np.ascontiguousarray(byte.astype(np.uint8).reshape(k // 512, 16, n))


def unpack_weight(words, scales, fmt):
    g, p, n, _ = words.shape
    if fmt == "e4m3":
        vals = np.ascontiguousarray(words).view(ml_dtypes.float8_e4m3fn).astype(np.float64)
    else:
        nib = np.empty((g, p, n, 4), np.uint8)
        nib[..., 0::2] = words & 0xF
        nib[..., 1::2] = words >> 4
        vals = E2M1[nib]
    vals = vals * np.repeat(np.exp2(scales.astype(np.float64) - 127.0), 8, axis=1)[..., None]
    return vals.transpose(0, 1, 3, 2).reshape(g * 512, n)

def pack4(w):
    words, scales = pack_weight(w, "e2m1")
    return words.reshape(words.shape[0], 128, -1), scales


def unpack4(words, scales):
    return unpack_weight(words.reshape(words.shape[0], 128, -1, 2), scales, "e2m1")


B, S, D, BD, K = 4, 1024, 1024, 512, 128
TS = 3.0


def sigmoid(v):
    return 1.0 / (1.0 + np.exp(-v))


def setup_inputs():
    s = mx_kscale(D)
    token_embeddings = bf(np.random.standard_normal((B, S, D)) * TS * s)
    splat_influences = bf(np.random.uniform(size=(B, S, K)))
    decoded = bf(np.random.standard_normal((B, K, D)) * 0.35)
    gate_W_words, gate_W_scales = pack4(np.random.standard_normal((D, D)) / (TS * np.sqrt(D)) / s[:, None])
    gate_b = bf(np.random.standard_normal(D) * 0.5)
    return {
        "token_embeddings": token_embeddings,
        "splat_influences": splat_influences,
        "decoded": decoded,
        "gate_W_words": gate_W_words,
        "gate_W_scales": gate_W_scales,
        "gate_b": gate_b,
    }


def reference(token_embeddings, splat_influences, decoded, gate_W_words, gate_W_scales, gate_b):
    flow = f64(splat_influences) @ f64(decoded)
    gate = sigmoid((mxq(f64(token_embeddings), 2, "e4m3") @ unpack4(gate_W_words, gate_W_scales)) + f64(gate_b))
    return flow * gate

@@ -1,0 +1,203 @@
+from contextlib import ExitStack
+
+import concourse.mybir as mybir
+from concourse.masks import make_identity
+
+F32 = mybir.dt.float32
+BF16 = mybir.dt.bfloat16
+I32 = mybir.dt.int32
+U32 = mybir.dt.uint32
+U8 = mybir.dt.uint8
+FP8X4 = mybir.dt.float8_e4m3fn_x4
+FP4X4 = mybir.dt.float4_e2m1fn_x4
+ADD = mybir.AluOpType.add
+MULT = mybir.AluOpType.mult
+SIGMOID = mybir.ActivationFunctionType.Sigmoid
+
+P = 128
+BATCHES = 4
+TOKENS = 1024
+D = 1024
+SPLATS = 128
+TILES_PER_BATCH = TOKENS // P
+N_TILES = BATCHES * TILES_PER_BATCH
+PAIR = 2
+N_PAIRS = N_TILES // PAIR
+PAIRS_PER_BATCH = TILES_PER_BATCH // PAIR
+K_PASS = 4 * P
+PASSES = D // K_PASS
+WORDS_PER_PASS = K_PASS // 2
+N_TILE = 512
+HALVES = D // N_TILE
+
+FLOPS = 2 * BATCHES * TOKENS * D * D + 2 * BATCHES * TOKENS * SPLATS * D
+
+
+def tile_splatinformationflow_pb_kernel(
+    tc, token_embeddings, splat_influences, decoded, gate_W_words, gate_W_scales, gate_b, out
+):
+    nc = tc.nc
+    with ExitStack() as ctx:
+        const = ctx.enter_context(tc.tile_pool(name="const", bufs=1))
+        x_pool = ctx.enter_context(tc.tile_pool(name="x", bufs=N_PAIRS))
+        batch_pool = ctx.enter_context(tc.tile_pool(name="batch", bufs=BATCHES))
+        grouped_pool = ctx.enter_context(tc.tile_pool(name="grouped", bufs=2))
+        mx_pool = ctx.enter_context(tc.tile_pool(name="mx", bufs=3))
+        gate_pool = ctx.enter_context(tc.tile_pool(name="gate", bufs=3))
+        out_pool = ctx.enter_context(tc.tile_pool(name="outs", bufs=8))
+        psum_gate = ctx.enter_context(tc.psum_pool(name="psum_gate", bufs=3))
+        psum_flow = ctx.enter_context(tc.psum_pool(name="psum_flow", bufs=2))
+        psum_xt = ctx.enter_context(tc.psum_pool(name="psum_xt", bufs=2))
+        psum_it = ctx.enter_context(tc.psum_pool(name="psum_it", bufs=1))
+        ctx.enter_context(tc.manual_schedule())
+
+        x_view = token_embeddings.rearrange("b (p j) k -> b p j k", j=TILES_PER_BATCH)
+        infl_view = splat_influences.rearrange("b (p j) s -> b p j s", j=TILES_PER_BATCH)
+        out_view = out.rearrange("b (p j) d -> b p j d", j=TILES_PER_BATCH)
+
+        x_sb = []
+        infl_sb = []
+        dec_sb = []
+
+        def load_x_pair(m):
+            b, q = divmod(m, PAIRS_PER_BATCH)
+            x_pair = x_pool.tile([P, PAIR, D], BF16)
+            nc.sync.dma_start(out=x_pair[:], in_=x_view[b, :, q * PAIR : (q + 1) * PAIR, :])
+            x_sb.append(x_pair)
+
+        def load_flow_operands(b):
+            infl = batch_pool.tile([P, TILES_PER_BATCH, SPLATS], BF16)
+            nc.sync.dma_start(out=infl[:], in_=infl_view[b])
+            infl_sb.append(infl)
+            dec = batch_pool.tile([SPLATS, D], BF16)
+            nc.sync.dma_start(out=dec[:], in_=decoded[b])
+            dec_sb.append(dec)
+
+        bias_rows = const.tile([P, D], BF16)
+        nc.vector.memset(bias_rows[:], 0.0)
+        w_scales = const.tile([P, PASSES, D], U8, align_bytes=64)
+        nc.vector.memset(w_scales[:].rearrange("p g n -> p (g n)").bitcast(I32), 0)
+        ones = const.tile([P, P], BF16)
+        nc.vector.memset(ones[:], 1.0)
+        warm = const.tile([P, 1], F32)
+        nc.vector.memset(warm[:], 0.0)
+        nc.scalar.activation(out=warm[:], in_=warm[:], func=SIGMOID)
+
+        ident_f32 = const.tile([P, P], F32)
+        make_identity(nc, ident_f32[:])
+        ident_bf16 = const.tile([P, P], BF16)
+        make_identity(nc, ident_bf16[:])
+
+        load_x_pair(0)
+        w_words = const.tile([P, PASSES, 2 * D], U8, align_bytes=64)
+        nc.sync.dma_start(out=w_words[:].bitcast(I32), in_=gate_W_words.bitcast(I32).rearrange("g p w -> p g w"))
+        nc.sync.dma_start(out=bias_rows[0:1, :], in_=gate_b.unsqueeze(0))
+        for r in range(4):
+            nc.sync.dma_start(
+                out=w_scales[:].bitcast(I32)[r:P:32],
+                in_=gate_W_scales.bitcast(I32)[:, r:16:4, :].rearrange("g q n -> q g n"),
+            )
+        for b in range(BATCHES):
+            load_flow_operands(b)
+            for q in range(PAIRS_PER_BATCH):
+                if b * PAIRS_PER_BATCH + q > 0:
+                    load_x_pair(b * PAIRS_PER_BATCH + q)
+
+        infl_t_sb = []
+        grouped_sb = []
+        x_codes = []
+        x_scales = []
+        gates = []
+
+        bias_f32 = const.tile([P, D], F32)
+
+        def broadcast_bias():
+            for h in range(HALVES):
+                cols = slice(h * N_TILE, (h + 1) * N_TILE)
+                bias_ps = psum_gate.tile([P, N_TILE], F32, tag="gate_ps")
+                nc.tensor.matmul(bias_ps[:], lhsT=ones[:], rhs=bias_rows[:, cols], start=True, stop=True)
+                nc.vector.tensor_copy(out=bias_f32[:, cols], in_=bias_ps[:])
+
+        def transpose_influences(b):
+            it_ps = psum_it.tile([SPLATS, TILES_PER_BATCH, P], BF16)
+            for j in range(TILES_PER_BATCH):
+                nc.tensor.transpose(it_ps[:, j, :], infl_sb[b][:, j, :], ident_bf16[:])
+            infl_t = batch_pool.tile([SPLATS, TILES_PER_BATCH, P], BF16)
+            nc.scalar.copy(out=infl_t[:], in_=it_ps[:])
+            infl_t_sb.append(infl_t)
+
+        def transpose_pair(m):
+            grouped = grouped_pool.tile([P, PAIR, D], BF16, align_bytes=64)
+            x_words = x_sb[m][:].bitcast(F32)
+            for a in range(PAIR):
+                xt_ps = psum_xt.tile([P, PASSES * 2, P], F32)
+                for g in range(PASSES):
+                    for u in range(2):
+                        nc.tensor.transpose(
+                            xt_ps[:, 2 * g + u, :],
+                            x_words[:, a, g * WORDS_PER_PASS + u : (g + 1) * WORDS_PER_PASS : 2],
+                            ident_f32[:],
+                        )
+                nc.scalar.copy(
+                    out=grouped[:, a, :].bitcast(F32).rearrange("p (g r u) -> p g r u", g=PASSES, u=2),
+                    in_=xt_ps[:].rearrange("p (g u) r -> p g r u", u=2),
+                )
+            grouped_sb.append(grouped)
+
+        def quantise_pair(m):
+            codes = mx_pool.tile([P, PAIR * PASSES, P], U32, align_bytes=64)
+            scales = mx_pool.tile([P, PAIR * PASSES, P], U8, align_bytes=64)
+            nc.vector.quantize_mx(
+                out=codes[:].rearrange("p s r -> p (s r)").bitcast(FP8X4),
+                scales=scales[:].rearrange("p s r -> p (s r)"),
+                in_=grouped_sb[m][:].rearrange("p a c -> p (a c)"),
+            )
+            x_codes.append(codes)
+            x_scales.append(scales)
+
+        def gate(i):
+            m, a = divmod(i, PAIR)
+            gate_sb = gate_pool.tile([P, D], F32)
+            for h in range(HALVES):
+                cols = slice(h * N_TILE, (h + 1) * N_TILE)
+                gate_ps = psum_gate.tile([P, N_TILE], F32, tag="gate_ps")
+                for g in range(PASSES):
+                    nc.tensor.matmul_mx(
+                        out=gate_ps[:],
+                        lhsT=x_codes[m][:, a * PASSES + g, :].bitcast(FP8X4),
+                        lhsT_scale=x_scales[m][:, a * PASSES + g, :],
+                        rhs=w_words[:, g, 2 * h * N_TILE : 2 * (h + 1) * N_TILE].bitcast(FP4X4),
+                        rhs_scale=w_scales[:, g, cols],
+                        start=(g == 0),
+                        stop=(g == PASSES - 1),
+                    )
+                nc.vector.tensor_tensor(out=gate_sb[:, cols], in0=gate_ps[:], in1=bias_f32[:, cols], op=ADD)
+            nc.scalar.activation(out=gate_sb[:], in_=gate_sb[:], func=SIGMOID)
+            gates.append(gate_sb)
+
+        def flow_and_store(i):
+            b, j = divmod(i, TILES_PER_BATCH)
+            out_sb = out_pool.tile([P, D], F32)
+            for h in range(HALVES):
+                cols = slice(h * N_TILE, (h + 1) * N_TILE)
+                flow_ps = psum_flow.tile([P, N_TILE], F32)
+                nc.tensor.matmul(flow_ps[:], lhsT=infl_t_sb[b][:, j, :], rhs=dec_sb[b][:, cols], start=True, stop=True)
+                nc.vector.tensor_tensor(out=out_sb[:, cols], in0=flow_ps[:], in1=gates[i][:, cols], op=MULT)
+            nc.sync.dma_start(out=out_view[b, :, j, :], in_=out_sb[:])
+
+        transpose_pair(0)
+        quantise_pair(0)
+        broadcast_bias()
+        transpose_influences(0)
+        transpose_pair(1)
+        for i in range(N_TILES):
+            gate(i)
+            if i % PAIR == 1 and (i + 3) // PAIR < N_PAIRS:
+                transpose_pair((i + 3) // PAIR)
+            if i % TILES_PER_BATCH == TILES_PER_BATCH - 1 and i + 1 < N_TILES:
+                transpose_influences((i + 1) // TILES_PER_BATCH)
+            if i > 0:
+                flow_and_store(i - 1)
+            if i % PAIR == 0 and i // PAIR + 1 < N_PAIRS:
+                quantise_pair(i // PAIR + 1)
+        flow_and_store(N_TILES - 1)

@@ -44,6 +44,7 @@ def tile_splatinformationflow_pb_kernel(
         grouped_pool = ctx.enter_context(tc.tile_pool(name="grouped", bufs=2))
         mx_pool = ctx.enter_context(tc.tile_pool(name="mx", bufs=3))
         gate_pool = ctx.enter_context(tc.tile_pool(name="gate", bufs=3))
+        flow_pool = ctx.enter_context(tc.tile_pool(name="flow", bufs=3))
         out_pool = ctx.enter_context(tc.tile_pool(name="outs", bufs=8))
         psum_gate = ctx.enter_context(tc.psum_pool(name="psum_gate", bufs=3))
         psum_flow = ctx.enter_context(tc.psum_pool(name="psum_flow", bufs=2))
@@ -104,6 +105,7 @@ def tile_splatinformationflow_pb_kernel(
                     load_x_pair(b * PAIRS_PER_BATCH + q)
 
         infl_t_sb = []
+        xt_banks = []
         grouped_sb = []
         x_codes = []
         x_scales = []
@@ -138,11 +140,15 @@ def tile_splatinformationflow_pb_kernel(
                             x_words[:, a, g * WORDS_PER_PASS + u : (g + 1) * WORDS_PER_PASS : 2],
                             ident_f32[:],
                         )
-                nc.scalar.copy(
-                    out=grouped[:, a, :].bitcast(F32).rearrange("p (g r u) -> p g r u", g=PASSES, u=2),
-                    in_=xt_ps[:].rearrange("p (g u) r -> p g r u", u=2),
-                )
+                xt_banks.append(xt_ps)
             grouped_sb.append(grouped)
+
+        def regroup(i, copy):
+            m, a = divmod(i, PAIR)
+            copy(
+                out=grouped_sb[m][:, a, :].bitcast(F32).rearrange("p (g r u) -> p g r u", g=PASSES, u=2),
+                in_=xt_banks[i][:].rearrange("p (g u) r -> p g r u", u=2),
+            )
 
         def quantise_pair(m):
             codes = mx_pool.tile([P, PAIR * PASSES, P], U32, align_bytes=64)
@@ -182,22 +188,34 @@ def tile_splatinformationflow_pb_kernel(
                 cols = slice(h * N_TILE, (h + 1) * N_TILE)
                 flow_ps = psum_flow.tile([P, N_TILE], F32)
                 nc.tensor.matmul(flow_ps[:], lhsT=infl_t_sb[b][:, j, :], rhs=dec_sb[b][:, cols], start=True, stop=True)
-                nc.vector.tensor_tensor(out=out_sb[:, cols], in0=flow_ps[:], in1=gates[i][:, cols], op=MULT)
+                if h == 0:
+                    nc.vector.tensor_tensor(out=out_sb[:, cols], in0=flow_ps[:], in1=gates[i][:, cols], op=MULT)
+                else:
+                    flow_sb = flow_pool.tile([P, N_TILE], F32)
+                    nc.scalar.copy(out=flow_sb[:], in_=flow_ps[:])
+                    nc.gpsimd.tensor_tensor(out=out_sb[:, cols], in0=flow_sb[:], in1=gates[i][:, cols], op=MULT)
             nc.sync.dma_start(out=out_view[b, :, j, :], in_=out_sb[:])
 
         transpose_pair(0)
+        regroup(0, nc.scalar.copy)
+        regroup(1, nc.vector.tensor_copy)
         quantise_pair(0)
         broadcast_bias()
         transpose_influences(0)
         transpose_pair(1)
+        regroup(2, nc.scalar.copy)
+        regroup(3, nc.vector.tensor_copy)
         for i in range(N_TILES):
             gate(i)
-            if i % PAIR == 1 and (i + 3) // PAIR < N_PAIRS:
+            if i % PAIR == 1 and i + 3 < N_TILES:
                 transpose_pair((i + 3) // PAIR)
+                regroup(i + 3, nc.scalar.copy)
             if i % TILES_PER_BATCH == TILES_PER_BATCH - 1 and i + 1 < N_TILES:
                 transpose_influences((i + 1) // TILES_PER_BATCH)
             if i > 0:
                 flow_and_store(i - 1)
+            if i % PAIR == 1 and i + 3 < N_TILES:
+                regroup(i + 4, nc.vector.tensor_copy)
             if i % PAIR == 0 and i // PAIR + 1 < N_PAIRS:
                 quantise_pair(i // PAIR + 1)
         flow_and_store(N_TILES - 1)

@@ -20,17 +20,23 @@ TOKENS = 1024
 D = 1024
 SPLATS = 128
 TILES_PER_BATCH = TOKENS // P
-N_TILES = BATCHES * TILES_PER_BATCH
 PAIR = 2
-N_PAIRS = N_TILES // PAIR
 PAIRS_PER_BATCH = TILES_PER_BATCH // PAIR
+N_PAIRS = BATCHES * PAIRS_PER_BATCH
 K_PASS = 4 * P
 PASSES = D // K_PASS
 WORDS_PER_PASS = K_PASS // 2
 N_TILE = 512
 HALVES = D // N_TILE
+GPSIMD_HALF = 0
+VECTOR_HALF = 1
+PSUM_BANKS = 8
 
 FLOPS = 2 * BATCHES * TOKENS * D * D + 2 * BATCHES * TOKENS * SPLATS * D
+
+
+def half_cols(h):
+    return slice(h * N_TILE, (h + 1) * N_TILE)
 
 
 def tile_splatinformationflow_pb_kernel(
@@ -41,20 +47,31 @@ def tile_splatinformationflow_pb_kernel(
         const = ctx.enter_context(tc.tile_pool(name="const", bufs=1))
         x_pool = ctx.enter_context(tc.tile_pool(name="x", bufs=N_PAIRS))
         batch_pool = ctx.enter_context(tc.tile_pool(name="batch", bufs=BATCHES))
-        grouped_pool = ctx.enter_context(tc.tile_pool(name="grouped", bufs=2))
-        mx_pool = ctx.enter_context(tc.tile_pool(name="mx", bufs=3))
-        gate_pool = ctx.enter_context(tc.tile_pool(name="gate", bufs=3))
-        flow_pool = ctx.enter_context(tc.tile_pool(name="flow", bufs=3))
+        grouped_pool = ctx.enter_context(tc.tile_pool(name="grouped", bufs=PAIRS_PER_BATCH))
+        mx_pool = ctx.enter_context(tc.tile_pool(name="mx", bufs=2 * PAIRS_PER_BATCH))
+        gate_pool = ctx.enter_context(tc.tile_pool(name="gate", bufs=4))
+        flow_pool = ctx.enter_context(tc.tile_pool(name="flow", bufs=4))
         out_pool = ctx.enter_context(tc.tile_pool(name="outs", bufs=8))
-        psum_gate = ctx.enter_context(tc.psum_pool(name="psum_gate", bufs=3))
-        psum_flow = ctx.enter_context(tc.psum_pool(name="psum_flow", bufs=2))
-        psum_xt = ctx.enter_context(tc.psum_pool(name="psum_xt", bufs=2))
-        psum_it = ctx.enter_context(tc.psum_pool(name="psum_it", bufs=1))
+        psum = ctx.enter_context(tc.psum_pool(name="psum", bufs=PSUM_BANKS))
         ctx.enter_context(tc.manual_schedule())
 
         x_view = token_embeddings.rearrange("b (p j) k -> b p j k", j=TILES_PER_BATCH)
         infl_view = splat_influences.rearrange("b (p j) s -> b p j s", j=TILES_PER_BATCH)
         out_view = out.rearrange("b (p j) d -> b p j d", j=TILES_PER_BATCH)
+
+        bias_rows = const.tile([P, D], BF16)
+        nc.vector.memset(bias_rows[:], 0.0)
+        w_scales = const.tile([P, PASSES, D], U8, align_bytes=64)
+        nc.vector.memset(w_scales[:].rearrange("p g n -> p (g n)").bitcast(I32), 0)
+        ones = const.tile([P, P], BF16)
+        nc.vector.memset(ones[:], 1.0)
+        warm = const.tile([P, 1], F32)
+        nc.vector.memset(warm[:], 0.0)
+        nc.scalar.activation(out=warm[:], in_=warm[:], func=SIGMOID)
+        ident_f32 = const.tile([P, P], F32)
+        make_identity(nc, ident_f32[:])
+        ident_bf16 = const.tile([P, P], BF16)
+        make_identity(nc, ident_bf16[:])
 
         x_sb = []
         infl_sb = []
@@ -74,35 +91,25 @@ def tile_splatinformationflow_pb_kernel(
             nc.sync.dma_start(out=dec[:], in_=decoded[b])
             dec_sb.append(dec)
 
-        bias_rows = const.tile([P, D], BF16)
-        nc.vector.memset(bias_rows[:], 0.0)
-        w_scales = const.tile([P, PASSES, D], U8, align_bytes=64)
-        nc.vector.memset(w_scales[:].rearrange("p g n -> p (g n)").bitcast(I32), 0)
-        ones = const.tile([P, P], BF16)
-        nc.vector.memset(ones[:], 1.0)
-        warm = const.tile([P, 1], F32)
-        nc.vector.memset(warm[:], 0.0)
-        nc.scalar.activation(out=warm[:], in_=warm[:], func=SIGMOID)
-
-        ident_f32 = const.tile([P, P], F32)
-        make_identity(nc, ident_f32[:])
-        ident_bf16 = const.tile([P, P], BF16)
-        make_identity(nc, ident_bf16[:])
-
-        load_x_pair(0)
         w_words = const.tile([P, PASSES, 2 * D], U8, align_bytes=64)
-        nc.sync.dma_start(out=w_words[:].bitcast(I32), in_=gate_W_words.bitcast(I32).rearrange("g p w -> p g w"))
-        nc.sync.dma_start(out=bias_rows[0:1, :], in_=gate_b.unsqueeze(0))
-        for r in range(4):
-            nc.sync.dma_start(
-                out=w_scales[:].bitcast(I32)[r:P:32],
-                in_=gate_W_scales.bitcast(I32)[:, r:16:4, :].rearrange("g q n -> q g n"),
-            )
+
+        def load_gate_weights():
+            nc.sync.dma_start(out=w_words[:].bitcast(I32), in_=gate_W_words.bitcast(I32).rearrange("g p w -> p g w"))
+            nc.sync.dma_start(out=bias_rows[0:1, :], in_=gate_b.unsqueeze(0))
+            for r in range(4):
+                nc.sync.dma_start(
+                    out=w_scales[:].bitcast(I32)[r:P:32],
+                    in_=gate_W_scales.bitcast(I32)[:, r:16:4, :].rearrange("g q n -> q g n"),
+                )
+
         for b in range(BATCHES):
+            load_x_pair(b * PAIRS_PER_BATCH)
+            load_x_pair(b * PAIRS_PER_BATCH + 1)
             load_flow_operands(b)
-            for q in range(PAIRS_PER_BATCH):
-                if b * PAIRS_PER_BATCH + q > 0:
-                    load_x_pair(b * PAIRS_PER_BATCH + q)
+            load_x_pair(b * PAIRS_PER_BATCH + 2)
+            load_x_pair(b * PAIRS_PER_BATCH + 3)
+            if b == 0:
+                load_gate_weights()
 
         infl_t_sb = []
         xt_banks = []
@@ -110,18 +117,19 @@ def tile_splatinformationflow_pb_kernel(
         x_codes = []
         x_scales = []
         gates = []
+        flows = []
+        outs = []
 
         bias_f32 = const.tile([P, D], F32)
 
         def broadcast_bias():
             for h in range(HALVES):
-                cols = slice(h * N_TILE, (h + 1) * N_TILE)
-                bias_ps = psum_gate.tile([P, N_TILE], F32, tag="gate_ps")
-                nc.tensor.matmul(bias_ps[:], lhsT=ones[:], rhs=bias_rows[:, cols], start=True, stop=True)
-                nc.vector.tensor_copy(out=bias_f32[:, cols], in_=bias_ps[:])
+                bias_ps = psum.tile([P, N_TILE], F32, tag="bank")
+                nc.tensor.matmul(bias_ps[:], lhsT=ones[:], rhs=bias_rows[:, half_cols(h)], start=True, stop=True)
+                nc.vector.tensor_copy(out=bias_f32[:, half_cols(h)], in_=bias_ps[:])
 
         def transpose_influences(b):
-            it_ps = psum_it.tile([SPLATS, TILES_PER_BATCH, P], BF16)
+            it_ps = psum.tile([SPLATS, TILES_PER_BATCH, P], BF16, tag="bank")
             for j in range(TILES_PER_BATCH):
                 nc.tensor.transpose(it_ps[:, j, :], infl_sb[b][:, j, :], ident_bf16[:])
             infl_t = batch_pool.tile([SPLATS, TILES_PER_BATCH, P], BF16)
@@ -130,9 +138,10 @@ def tile_splatinformationflow_pb_kernel(
 
         def transpose_pair(m):
             grouped = grouped_pool.tile([P, PAIR, D], BF16, align_bytes=64)
+            grouped_sb.append(grouped)
             x_words = x_sb[m][:].bitcast(F32)
             for a in range(PAIR):
-                xt_ps = psum_xt.tile([P, PASSES * 2, P], F32)
+                xt_ps = psum.tile([P, PASSES * 2, P], F32, tag="bank")
                 for g in range(PASSES):
                     for u in range(2):
                         nc.tensor.transpose(
@@ -141,7 +150,6 @@ def tile_splatinformationflow_pb_kernel(
                             ident_f32[:],
                         )
                 xt_banks.append(xt_ps)
-            grouped_sb.append(grouped)
 
         def regroup(i, copy):
             m, a = divmod(i, PAIR)
@@ -161,61 +169,81 @@ def tile_splatinformationflow_pb_kernel(
             x_codes.append(codes)
             x_scales.append(scales)
 
-        def gate(i):
+        def prepare(b):
+            for q in range(PAIRS_PER_BATCH):
+                m = b * PAIRS_PER_BATCH + q
+                transpose_pair(m)
+                regroup(m * PAIR, nc.scalar.copy)
+                regroup(m * PAIR + 1, nc.vector.tensor_copy)
+                if q == 1:
+                    transpose_influences(b)
+                if q > 0:
+                    quantise_pair(m - 1)
+            quantise_pair(b * PAIRS_PER_BATCH + PAIRS_PER_BATCH - 1)
+
+        def flow(i, h):
+            b, j = divmod(i, TILES_PER_BATCH)
+            flow_ps = psum.tile([P, N_TILE], F32, tag="bank")
+            nc.tensor.matmul(
+                flow_ps[:], lhsT=infl_t_sb[b][:, j, :], rhs=dec_sb[b][:, half_cols(h)], start=True, stop=True
+            )
+            return flow_ps
+
+        def flow_for_gpsimd(i):
+            flow_ps = flow(i, GPSIMD_HALF)
+            flow_sb = flow_pool.tile([P, N_TILE], F32)
+            nc.scalar.copy(out=flow_sb[:], in_=flow_ps[:])
+            flows.append(flow_sb)
+
+        def gate_sums(i):
             m, a = divmod(i, PAIR)
             gate_sb = gate_pool.tile([P, D], F32)
             for h in range(HALVES):
-                cols = slice(h * N_TILE, (h + 1) * N_TILE)
-                gate_ps = psum_gate.tile([P, N_TILE], F32, tag="gate_ps")
+                gate_ps = psum.tile([P, N_TILE], F32, tag="bank")
                 for g in range(PASSES):
                     nc.tensor.matmul_mx(
                         out=gate_ps[:],
                         lhsT=x_codes[m][:, a * PASSES + g, :].bitcast(FP8X4),
                         lhsT_scale=x_scales[m][:, a * PASSES + g, :],
                         rhs=w_words[:, g, 2 * h * N_TILE : 2 * (h + 1) * N_TILE].bitcast(FP4X4),
-                        rhs_scale=w_scales[:, g, cols],
+                        rhs_scale=w_scales[:, g, half_cols(h)],
                         start=(g == 0),
                         stop=(g == PASSES - 1),
                     )
-                nc.vector.tensor_tensor(out=gate_sb[:, cols], in0=gate_ps[:], in1=bias_f32[:, cols], op=ADD)
-            nc.scalar.activation(out=gate_sb[:], in_=gate_sb[:], func=SIGMOID)
+                nc.vector.tensor_tensor(
+                    out=gate_sb[:, half_cols(h)], in0=gate_ps[:], in1=bias_f32[:, half_cols(h)], op=ADD
+                )
             gates.append(gate_sb)
 
-        def flow_and_store(i):
-            b, j = divmod(i, TILES_PER_BATCH)
-            out_sb = out_pool.tile([P, D], F32)
-            for h in range(HALVES):
-                cols = slice(h * N_TILE, (h + 1) * N_TILE)
-                flow_ps = psum_flow.tile([P, N_TILE], F32)
-                nc.tensor.matmul(flow_ps[:], lhsT=infl_t_sb[b][:, j, :], rhs=dec_sb[b][:, cols], start=True, stop=True)
-                if h == 0:
-                    nc.vector.tensor_tensor(out=out_sb[:, cols], in0=flow_ps[:], in1=gates[i][:, cols], op=MULT)
-                else:
-                    flow_sb = flow_pool.tile([P, N_TILE], F32)
-                    nc.scalar.copy(out=flow_sb[:], in_=flow_ps[:])
-                    nc.gpsimd.tensor_tensor(out=out_sb[:, cols], in0=flow_sb[:], in1=gates[i][:, cols], op=MULT)
-            nc.sync.dma_start(out=out_view[b, :, j, :], in_=out_sb[:])
+        def sigmoid(i, h):
+            nc.scalar.activation(out=gates[i][:, half_cols(h)], in_=gates[i][:, half_cols(h)], func=SIGMOID)
 
-        transpose_pair(0)
-        regroup(0, nc.scalar.copy)
-        regroup(1, nc.vector.tensor_copy)
-        quantise_pair(0)
-        broadcast_bias()
-        transpose_influences(0)
-        transpose_pair(1)
-        regroup(2, nc.scalar.copy)
-        regroup(3, nc.vector.tensor_copy)
-        for i in range(N_TILES):
-            gate(i)
-            if i % PAIR == 1 and i + 3 < N_TILES:
-                transpose_pair((i + 3) // PAIR)
-                regroup(i + 3, nc.scalar.copy)
-            if i % TILES_PER_BATCH == TILES_PER_BATCH - 1 and i + 1 < N_TILES:
-                transpose_influences((i + 1) // TILES_PER_BATCH)
-            if i > 0:
-                flow_and_store(i - 1)
-            if i % PAIR == 1 and i + 3 < N_TILES:
-                regroup(i + 4, nc.vector.tensor_copy)
-            if i % PAIR == 0 and i // PAIR + 1 < N_PAIRS:
-                quantise_pair(i // PAIR + 1)
-        flow_and_store(N_TILES - 1)
+        def gpsimd_product(i):
+            out_sb = out_pool.tile([P, D], F32)
+            cols = half_cols(GPSIMD_HALF)
+            nc.gpsimd.tensor_tensor(out=out_sb[:, cols], in0=flows[i][:], in1=gates[i][:, cols], op=MULT)
+            outs.append(out_sb)
+
+        def vector_product_and_store(i):
+            b, j = divmod(i, TILES_PER_BATCH)
+            cols = half_cols(VECTOR_HALF)
+            flow_ps = flow(i, VECTOR_HALF)
+            nc.vector.tensor_tensor(out=outs[i][:, cols], in0=flow_ps[:], in1=gates[i][:, cols], op=MULT)
+            nc.sync.dma_start(out=out_view[b, :, j, :], in_=outs[i][:])
+
+        for b in range(BATCHES):
+            prepare(b)
+            if b == 0:
+                broadcast_bias()
+            first = b * TILES_PER_BATCH
+            for j in range(TILES_PER_BATCH + 1):
+                i = first + j
+                if j < TILES_PER_BATCH:
+                    flow_for_gpsimd(i)
+                    gate_sums(i)
+                if j > 0:
+                    vector_product_and_store(i - 1)
+                if j < TILES_PER_BATCH:
+                    sigmoid(i, GPSIMD_HALF)
+                    gpsimd_product(i)
+                    sigmoid(i, VECTOR_HALF)

@@ -20,6 +20,7 @@ TOKENS = 1024
 D = 1024
 SPLATS = 128
 TILES_PER_BATCH = TOKENS // P
+N_TILES = BATCHES * TILES_PER_BATCH
 PAIR = 2
 PAIRS_PER_BATCH = TILES_PER_BATCH // PAIR
 N_PAIRS = BATCHES * PAIRS_PER_BATCH
@@ -231,19 +232,17 @@ def tile_splatinformationflow_pb_kernel(
             nc.vector.tensor_tensor(out=outs[i][:, cols], in0=flow_ps[:], in1=gates[i][:, cols], op=MULT)
             nc.sync.dma_start(out=out_view[b, :, j, :], in_=outs[i][:])
 
-        for b in range(BATCHES):
-            prepare(b)
-            if b == 0:
+        for i in range(N_TILES + 1):
+            if i < N_TILES and i % TILES_PER_BATCH == 0:
+                prepare(i // TILES_PER_BATCH)
+            if i == 0:
                 broadcast_bias()
-            first = b * TILES_PER_BATCH
-            for j in range(TILES_PER_BATCH + 1):
-                i = first + j
-                if j < TILES_PER_BATCH:
-                    flow_for_gpsimd(i)
-                    gate_sums(i)
-                if j > 0:
-                    vector_product_and_store(i - 1)
-                if j < TILES_PER_BATCH:
-                    sigmoid(i, GPSIMD_HALF)
-                    gpsimd_product(i)
-                    sigmoid(i, VECTOR_HALF)
+            if i < N_TILES:
+                flow_for_gpsimd(i)
+                gate_sums(i)
+            if i > 0:
+                vector_product_and_store(i - 1)
+            if i < N_TILES:
+                sigmoid(i, GPSIMD_HALF)
+                gpsimd_product(i)
+                sigmoid(i, VECTOR_HALF)

@@ -24,6 +24,7 @@ N_TILES = BATCHES * TILES_PER_BATCH
 PAIR = 2
 PAIRS_PER_BATCH = TILES_PER_BATCH // PAIR
 N_PAIRS = BATCHES * PAIRS_PER_BATCH
+LOAD_AHEAD = 6
 K_PASS = 4 * P
 PASSES = D // K_PASS
 WORDS_PER_PASS = K_PASS // 2
@@ -31,7 +32,9 @@ N_TILE = 512
 HALVES = D // N_TILE
 GPSIMD_HALF = 0
 VECTOR_HALF = 1
-PSUM_BANKS = 8
+TRANSPOSE_BANKS = 2
+GATE_BANKS = 4
+FLOW_BANKS = 2
 
 FLOPS = 2 * BATCHES * TOKENS * D * D + 2 * BATCHES * TOKENS * SPLATS * D
 
@@ -46,42 +49,47 @@ def tile_splatinformationflow_pb_kernel(
     nc = tc.nc
     with ExitStack() as ctx:
         const = ctx.enter_context(tc.tile_pool(name="const", bufs=1))
-        x_pool = ctx.enter_context(tc.tile_pool(name="x", bufs=N_PAIRS))
+        x_pool = ctx.enter_context(tc.tile_pool(name="x", bufs=LOAD_AHEAD + 2))
         batch_pool = ctx.enter_context(tc.tile_pool(name="batch", bufs=BATCHES))
-        grouped_pool = ctx.enter_context(tc.tile_pool(name="grouped", bufs=PAIRS_PER_BATCH))
-        mx_pool = ctx.enter_context(tc.tile_pool(name="mx", bufs=2 * PAIRS_PER_BATCH))
-        gate_pool = ctx.enter_context(tc.tile_pool(name="gate", bufs=4))
+        grouped_pool = ctx.enter_context(tc.tile_pool(name="grouped", bufs=3))
+        mx_pool = ctx.enter_context(tc.tile_pool(name="mx", bufs=4))
+        gate_pool = ctx.enter_context(tc.tile_pool(name="gate", bufs=5))
         flow_pool = ctx.enter_context(tc.tile_pool(name="flow", bufs=4))
-        out_pool = ctx.enter_context(tc.tile_pool(name="outs", bufs=8))
-        psum = ctx.enter_context(tc.psum_pool(name="psum", bufs=PSUM_BANKS))
+        out_pool = ctx.enter_context(tc.tile_pool(name="outs", bufs=10))
+        psum_t = ctx.enter_context(tc.psum_pool(name="psum_t", bufs=TRANSPOSE_BANKS))
+        psum_gate = ctx.enter_context(tc.psum_pool(name="psum_gate", bufs=GATE_BANKS))
+        psum_flow = ctx.enter_context(tc.psum_pool(name="psum_flow", bufs=FLOW_BANKS))
         ctx.enter_context(tc.manual_schedule())
 
         x_view = token_embeddings.rearrange("b (p j) k -> b p j k", j=TILES_PER_BATCH)
         infl_view = splat_influences.rearrange("b (p j) s -> b p j s", j=TILES_PER_BATCH)
         out_view = out.rearrange("b (p j) d -> b p j d", j=TILES_PER_BATCH)
 
-        bias_rows = const.tile([P, D], BF16)
-        nc.vector.memset(bias_rows[:], 0.0)
+        ident_f32 = const.tile([P, P], F32)
+        make_identity(nc, ident_f32[:])
+        ident_bf16 = const.tile([P, P], BF16)
+        make_identity(nc, ident_bf16[:])
         w_scales = const.tile([P, PASSES, D], U8, align_bytes=64)
         nc.vector.memset(w_scales[:].rearrange("p g n -> p (g n)").bitcast(I32), 0)
+        bias_rows = const.tile([P, D], BF16)
+        nc.vector.memset(bias_rows[:], 0.0)
         ones = const.tile([P, P], BF16)
         nc.vector.memset(ones[:], 1.0)
         warm = const.tile([P, 1], F32)
         nc.vector.memset(warm[:], 0.0)
         nc.scalar.activation(out=warm[:], in_=warm[:], func=SIGMOID)
-        ident_f32 = const.tile([P, P], F32)
-        make_identity(nc, ident_f32[:])
-        ident_bf16 = const.tile([P, P], BF16)
-        make_identity(nc, ident_bf16[:])
 
         x_sb = []
         infl_sb = []
         dec_sb = []
 
-        def load_x_pair(m):
+        def load_x_pair(m, pieces):
             b, q = divmod(m, PAIRS_PER_BATCH)
             x_pair = x_pool.tile([P, PAIR, D], BF16)
-            nc.sync.dma_start(out=x_pair[:], in_=x_view[b, :, q * PAIR : (q + 1) * PAIR, :])
+            width = PAIR // pieces
+            for a in range(0, PAIR, width):
+                j = q * PAIR + a
+                nc.sync.dma_start(out=x_pair[:, a : a + width, :], in_=x_view[b, :, j : j + width, :])
             x_sb.append(x_pair)
 
         def load_flow_operands(b):
@@ -96,28 +104,33 @@ def tile_splatinformationflow_pb_kernel(
 
         def load_gate_weights():
             nc.sync.dma_start(out=w_words[:].bitcast(I32), in_=gate_W_words.bitcast(I32).rearrange("g p w -> p g w"))
-            nc.sync.dma_start(out=bias_rows[0:1, :], in_=gate_b.unsqueeze(0))
             for r in range(4):
                 nc.sync.dma_start(
                     out=w_scales[:].bitcast(I32)[r:P:32],
                     in_=gate_W_scales.bitcast(I32)[:, r:16:4, :].rearrange("g q n -> q g n"),
                 )
+            nc.sync.dma_start(out=bias_rows[0:1, :], in_=gate_b.unsqueeze(0))
 
-        for b in range(BATCHES):
-            load_x_pair(b * PAIRS_PER_BATCH)
-            load_x_pair(b * PAIRS_PER_BATCH + 1)
-            load_flow_operands(b)
-            load_x_pair(b * PAIRS_PER_BATCH + 2)
-            load_x_pair(b * PAIRS_PER_BATCH + 3)
-            if b == 0:
-                load_gate_weights()
+        def load(m):
+            if m % PAIRS_PER_BATCH == 0 and m > 0:
+                load_flow_operands(m // PAIRS_PER_BATCH)
+            load_x_pair(m, 1)
+
+        load_x_pair(0, PAIR)
+        load_gate_weights()
+        load_x_pair(1, 1)
+        load_flow_operands(0)
+        for m in range(2, LOAD_AHEAD):
+            load(m)
 
         infl_t_sb = []
         xt_banks = []
         grouped_sb = []
         x_codes = []
         x_scales = []
+        gate_banks = {}
         gates = []
+        flow_banks = {}
         flows = []
         outs = []
 
@@ -125,12 +138,12 @@ def tile_splatinformationflow_pb_kernel(
 
         def broadcast_bias():
             for h in range(HALVES):
-                bias_ps = psum.tile([P, N_TILE], F32, tag="bank")
+                bias_ps = psum_flow.tile([P, N_TILE], F32, tag="flow")
                 nc.tensor.matmul(bias_ps[:], lhsT=ones[:], rhs=bias_rows[:, half_cols(h)], start=True, stop=True)
-                nc.vector.tensor_copy(out=bias_f32[:, half_cols(h)], in_=bias_ps[:])
+                nc.scalar.copy(out=bias_f32[:, half_cols(h)], in_=bias_ps[:])
 
         def transpose_influences(b):
-            it_ps = psum.tile([SPLATS, TILES_PER_BATCH, P], BF16, tag="bank")
+            it_ps = psum_flow.tile([SPLATS, TILES_PER_BATCH, P], BF16, tag="flow")
             for j in range(TILES_PER_BATCH):
                 nc.tensor.transpose(it_ps[:, j, :], infl_sb[b][:, j, :], ident_bf16[:])
             infl_t = batch_pool.tile([SPLATS, TILES_PER_BATCH, P], BF16)
@@ -142,7 +155,7 @@ def tile_splatinformationflow_pb_kernel(
             grouped_sb.append(grouped)
             x_words = x_sb[m][:].bitcast(F32)
             for a in range(PAIR):
-                xt_ps = psum.tile([P, PASSES * 2, P], F32, tag="bank")
+                xt_ps = psum_t.tile([P, PASSES * 2, P], F32, tag="xt")
                 for g in range(PASSES):
                     for u in range(2):
                         nc.tensor.transpose(
@@ -170,37 +183,23 @@ def tile_splatinformationflow_pb_kernel(
             x_codes.append(codes)
             x_scales.append(scales)
 
-        def prepare(b):
-            for q in range(PAIRS_PER_BATCH):
-                m = b * PAIRS_PER_BATCH + q
-                transpose_pair(m)
-                regroup(m * PAIR, nc.scalar.copy)
-                regroup(m * PAIR + 1, nc.vector.tensor_copy)
-                if q == 1:
-                    transpose_influences(b)
-                if q > 0:
-                    quantise_pair(m - 1)
-            quantise_pair(b * PAIRS_PER_BATCH + PAIRS_PER_BATCH - 1)
-
         def flow(i, h):
             b, j = divmod(i, TILES_PER_BATCH)
-            flow_ps = psum.tile([P, N_TILE], F32, tag="bank")
+            flow_ps = psum_flow.tile([P, N_TILE], F32, tag="flow")
             nc.tensor.matmul(
                 flow_ps[:], lhsT=infl_t_sb[b][:, j, :], rhs=dec_sb[b][:, half_cols(h)], start=True, stop=True
             )
-            return flow_ps
+            flow_banks[i, h] = flow_ps
 
-        def flow_for_gpsimd(i):
-            flow_ps = flow(i, GPSIMD_HALF)
+        def copy_flow(i):
             flow_sb = flow_pool.tile([P, N_TILE], F32)
-            nc.scalar.copy(out=flow_sb[:], in_=flow_ps[:])
+            nc.scalar.copy(out=flow_sb[:], in_=flow_banks[i, GPSIMD_HALF][:])
             flows.append(flow_sb)
 
         def gate_sums(i):
             m, a = divmod(i, PAIR)
-            gate_sb = gate_pool.tile([P, D], F32)
             for h in range(HALVES):
-                gate_ps = psum.tile([P, N_TILE], F32, tag="bank")
+                gate_ps = psum_gate.tile([P, N_TILE], F32, tag="gate")
                 for g in range(PASSES):
                     nc.tensor.matmul_mx(
                         out=gate_ps[:],
@@ -211,10 +210,15 @@ def tile_splatinformationflow_pb_kernel(
                         start=(g == 0),
                         stop=(g == PASSES - 1),
                     )
-                nc.vector.tensor_tensor(
-                    out=gate_sb[:, half_cols(h)], in0=gate_ps[:], in1=bias_f32[:, half_cols(h)], op=ADD
-                )
-            gates.append(gate_sb)
+                gate_banks[i, h] = gate_ps
+
+        def add_bias(i, h):
+            if h == 0:
+                gate_sb = gate_pool.tile([P, D], F32)
+                gates.append(gate_sb)
+            nc.vector.tensor_tensor(
+                out=gates[i][:, half_cols(h)], in0=gate_banks[i, h][:], in1=bias_f32[:, half_cols(h)], op=ADD
+            )
 
         def sigmoid(i, h):
             nc.scalar.activation(out=gates[i][:, half_cols(h)], in_=gates[i][:, half_cols(h)], func=SIGMOID)
@@ -228,21 +232,44 @@ def tile_splatinformationflow_pb_kernel(
         def vector_product_and_store(i):
             b, j = divmod(i, TILES_PER_BATCH)
             cols = half_cols(VECTOR_HALF)
-            flow_ps = flow(i, VECTOR_HALF)
-            nc.vector.tensor_tensor(out=outs[i][:, cols], in0=flow_ps[:], in1=gates[i][:, cols], op=MULT)
+            nc.vector.tensor_tensor(
+                out=outs[i][:, cols], in0=flow_banks[i, VECTOR_HALF][:], in1=gates[i][:, cols], op=MULT
+            )
             nc.sync.dma_start(out=out_view[b, :, j, :], in_=outs[i][:])
 
-        for i in range(N_TILES + 1):
-            if i < N_TILES and i % TILES_PER_BATCH == 0:
-                prepare(i // TILES_PER_BATCH)
-            if i == 0:
+        transpose_pair(0)
+        regroup(0, nc.scalar.copy)
+        regroup(1, nc.vector.tensor_copy)
+        quantise_pair(0)
+        for m in range(N_PAIRS):
+            if m + LOAD_AHEAD < N_PAIRS:
+                load(m + LOAD_AHEAD)
+            ahead = m + 1
+            if ahead < N_PAIRS:
+                transpose_pair(ahead)
+                regroup(ahead * PAIR, nc.scalar.copy)
+            if m == 0:
                 broadcast_bias()
-            if i < N_TILES:
-                flow_for_gpsimd(i)
+                transpose_influences(0)
+            if ahead % PAIRS_PER_BATCH == 0 and ahead < N_PAIRS:
+                transpose_influences(ahead // PAIRS_PER_BATCH)
+            for a in range(PAIR):
+                i = m * PAIR + a
+                flow(i, GPSIMD_HALF)
+                copy_flow(i)
                 gate_sums(i)
-            if i > 0:
-                vector_product_and_store(i - 1)
-            if i < N_TILES:
+                if i > 0:
+                    flow(i - 1, VECTOR_HALF)
+                add_bias(i, 0)
+                if a == 1 and ahead < N_PAIRS:
+                    quantise_pair(ahead)
+                add_bias(i, 1)
+                if a == 0 and ahead < N_PAIRS:
+                    regroup(ahead * PAIR + 1, nc.vector.tensor_copy)
+                if i > 0:
+                    vector_product_and_store(i - 1)
                 sigmoid(i, GPSIMD_HALF)
                 gpsimd_product(i)
                 sigmoid(i, VECTOR_HALF)
+        flow(N_TILES - 1, VECTOR_HALF)
+        vector_product_and_store(N_TILES - 1)

@@ -33,8 +33,8 @@ HALVES = D // N_TILE
 GPSIMD_HALF = 0
 VECTOR_HALF = 1
 TRANSPOSE_BANKS = 2
-GATE_BANKS = 4
-FLOW_BANKS = 2
+GATE_BANKS = 3
+FLOW_BANKS = 3
 
 FLOPS = 2 * BATCHES * TOKENS * D * D + 2 * BATCHES * TOKENS * SPLATS * D
 
@@ -65,14 +65,14 @@ def tile_splatinformationflow_pb_kernel(
         infl_view = splat_influences.rearrange("b (p j) s -> b p j s", j=TILES_PER_BATCH)
         out_view = out.rearrange("b (p j) d -> b p j d", j=TILES_PER_BATCH)
 
+        bias_rows = const.tile([P, D], BF16)
+        nc.vector.memset(bias_rows[:], 0.0)
         ident_f32 = const.tile([P, P], F32)
         make_identity(nc, ident_f32[:])
         ident_bf16 = const.tile([P, P], BF16)
         make_identity(nc, ident_bf16[:])
         w_scales = const.tile([P, PASSES, D], U8, align_bytes=64)
         nc.vector.memset(w_scales[:].rearrange("p g n -> p (g n)").bitcast(I32), 0)
-        bias_rows = const.tile([P, D], BF16)
-        nc.vector.memset(bias_rows[:], 0.0)
         ones = const.tile([P, P], BF16)
         nc.vector.memset(ones[:], 1.0)
         warm = const.tile([P, 1], F32)
@@ -109,7 +109,6 @@ def tile_splatinformationflow_pb_kernel(
                     out=w_scales[:].bitcast(I32)[r:P:32],
                     in_=gate_W_scales.bitcast(I32)[:, r:16:4, :].rearrange("g q n -> q g n"),
                 )
-            nc.sync.dma_start(out=bias_rows[0:1, :], in_=gate_b.unsqueeze(0))
 
         def load(m):
             if m % PAIRS_PER_BATCH == 0 and m > 0:
@@ -117,8 +116,9 @@ def tile_splatinformationflow_pb_kernel(
             load_x_pair(m, 1)
 
         load_x_pair(0, PAIR)
-        load_gate_weights()
+        nc.sync.dma_start(out=bias_rows[0:1, :], in_=gate_b.unsqueeze(0))
         load_x_pair(1, 1)
+        load_gate_weights()
         load_flow_operands(0)
         for m in range(2, LOAD_AHEAD):
             load(m)
@@ -237,39 +237,50 @@ def tile_splatinformationflow_pb_kernel(
             )
             nc.sync.dma_start(out=out_view[b, :, j, :], in_=outs[i][:])
 
+        def regroup_pair_on_scalar(m):
+            regroup(m * PAIR, nc.scalar.copy)
+            if m % 2 == 0:
+                regroup(m * PAIR + 1, nc.scalar.copy)
+
         transpose_pair(0)
         regroup(0, nc.scalar.copy)
         regroup(1, nc.vector.tensor_copy)
+        broadcast_bias()
+        transpose_pair(1)
         quantise_pair(0)
         for m in range(N_PAIRS):
             if m + LOAD_AHEAD < N_PAIRS:
                 load(m + LOAD_AHEAD)
             ahead = m + 1
             if ahead < N_PAIRS:
-                transpose_pair(ahead)
-                regroup(ahead * PAIR, nc.scalar.copy)
-            if m == 0:
-                broadcast_bias()
-                transpose_influences(0)
-            if ahead % PAIRS_PER_BATCH == 0 and ahead < N_PAIRS:
-                transpose_influences(ahead // PAIRS_PER_BATCH)
+                regroup_pair_on_scalar(ahead)
             for a in range(PAIR):
                 i = m * PAIR + a
-                flow(i, GPSIMD_HALF)
-                copy_flow(i)
                 gate_sums(i)
+                if i == 0:
+                    transpose_influences(0)
+                    flow(0, GPSIMD_HALF)
+                    copy_flow(0)
                 if i > 0:
                     flow(i - 1, VECTOR_HALF)
+                if i + 1 < N_TILES:
+                    flow(i + 1, GPSIMD_HALF)
                 add_bias(i, 0)
                 if a == 1 and ahead < N_PAIRS:
                     quantise_pair(ahead)
                 add_bias(i, 1)
-                if a == 0 and ahead < N_PAIRS:
+                if a == 0 and ahead < N_PAIRS and ahead % 2:
                     regroup(ahead * PAIR + 1, nc.vector.tensor_copy)
                 if i > 0:
                     vector_product_and_store(i - 1)
                 sigmoid(i, GPSIMD_HALF)
                 gpsimd_product(i)
+                if i + 1 < N_TILES:
+                    copy_flow(i + 1)
                 sigmoid(i, VECTOR_HALF)
+            if m + 2 < N_PAIRS:
+                if (m + 2) % PAIRS_PER_BATCH == 0:
+                    transpose_influences((m + 2) // PAIRS_PER_BATCH)
+                transpose_pair(m + 2)
         flow(N_TILES - 1, VECTOR_HALF)
         vector_product_and_store(N_TILES - 1)

@@ -28,6 +28,8 @@ LOAD_AHEAD = 6
 K_PASS = 4 * P
 PASSES = D // K_PASS
 WORDS_PER_PASS = K_PASS // 2
+FLOW_WIDTH = 256
+TILES_AHEAD = 4
 N_TILE = 512
 HALVES = D // N_TILE
 GPSIMD_HALF = 0
@@ -51,8 +53,8 @@ def tile_splatinformationflow_pb_kernel(
         const = ctx.enter_context(tc.tile_pool(name="const", bufs=1))
         x_pool = ctx.enter_context(tc.tile_pool(name="x", bufs=LOAD_AHEAD + 2))
         batch_pool = ctx.enter_context(tc.tile_pool(name="batch", bufs=BATCHES))
-        grouped_pool = ctx.enter_context(tc.tile_pool(name="grouped", bufs=3))
-        mx_pool = ctx.enter_context(tc.tile_pool(name="mx", bufs=4))
+        grouped_pool = ctx.enter_context(tc.tile_pool(name="grouped", bufs=4))
+        mx_pool = ctx.enter_context(tc.tile_pool(name="mx", bufs=6))
         gate_pool = ctx.enter_context(tc.tile_pool(name="gate", bufs=5))
         flow_pool = ctx.enter_context(tc.tile_pool(name="flow", bufs=4))
         out_pool = ctx.enter_context(tc.tile_pool(name="outs", bufs=10))
@@ -150,46 +152,53 @@ def tile_splatinformationflow_pb_kernel(
             nc.scalar.copy(out=infl_t[:], in_=it_ps[:])
             infl_t_sb.append(infl_t)
 
-        def transpose_pair(m):
-            grouped = grouped_pool.tile([P, PAIR, D], BF16, align_bytes=64)
-            grouped_sb.append(grouped)
+        def token_transposes(i):
+            m, a = divmod(i, PAIR)
             x_words = x_sb[m][:].bitcast(F32)
-            for a in range(PAIR):
-                xt_ps = psum_t.tile([P, PASSES * 2, P], F32, tag="xt")
-                for g in range(PASSES):
-                    for u in range(2):
-                        nc.tensor.transpose(
-                            xt_ps[:, 2 * g + u, :],
-                            x_words[:, a, g * WORDS_PER_PASS + u : (g + 1) * WORDS_PER_PASS : 2],
-                            ident_f32[:],
-                        )
-                xt_banks.append(xt_ps)
+            xt_ps = psum_t.tile([P, PASSES * 2, P], F32, tag="xt")
+            xt_banks.append(xt_ps)
+
+            def one(g, u):
+                nc.tensor.transpose(
+                    xt_ps[:, 2 * g + u, :],
+                    x_words[:, a, g * WORDS_PER_PASS + u : (g + 1) * WORDS_PER_PASS : 2],
+                    ident_f32[:],
+                )
+
+            return [lambda g=g, u=u: one(g, u) for g in range(PASSES) for u in range(2)]
 
         def regroup(i, copy):
-            m, a = divmod(i, PAIR)
+            grouped = grouped_pool.tile([P, D], BF16, align_bytes=64)
+            grouped_sb.append(grouped)
             copy(
-                out=grouped_sb[m][:, a, :].bitcast(F32).rearrange("p (g r u) -> p g r u", g=PASSES, u=2),
+                out=grouped[:].bitcast(F32).rearrange("p (g r u) -> p g r u", g=PASSES, u=2),
                 in_=xt_banks[i][:].rearrange("p (g u) r -> p g r u", u=2),
             )
 
-        def quantise_pair(m):
-            codes = mx_pool.tile([P, PAIR * PASSES, P], U32, align_bytes=64)
-            scales = mx_pool.tile([P, PAIR * PASSES, P], U8, align_bytes=64)
+        def quantise(i):
+            codes = mx_pool.tile([P, PASSES, P], U32, align_bytes=64)
+            scales = mx_pool.tile([P, PASSES, P], U8, align_bytes=64)
             nc.vector.quantize_mx(
-                out=codes[:].rearrange("p s r -> p (s r)").bitcast(FP8X4),
-                scales=scales[:].rearrange("p s r -> p (s r)"),
-                in_=grouped_sb[m][:].rearrange("p a c -> p (a c)"),
+                out=codes[:].rearrange("p g r -> p (g r)").bitcast(FP8X4),
+                scales=scales[:].rearrange("p g r -> p (g r)"),
+                in_=grouped_sb[i][:],
             )
             x_codes.append(codes)
             x_scales.append(scales)
 
-        def flow(i, h):
+        def flow_matmuls(i, h):
             b, j = divmod(i, TILES_PER_BATCH)
             flow_ps = psum_flow.tile([P, N_TILE], F32, tag="flow")
-            nc.tensor.matmul(
-                flow_ps[:], lhsT=infl_t_sb[b][:, j, :], rhs=dec_sb[b][:, half_cols(h)], start=True, stop=True
-            )
             flow_banks[i, h] = flow_ps
+
+            def one(c):
+                cols = slice(c * FLOW_WIDTH, (c + 1) * FLOW_WIDTH)
+                dec_cols = slice(h * N_TILE + c * FLOW_WIDTH, h * N_TILE + (c + 1) * FLOW_WIDTH)
+                nc.tensor.matmul(
+                    flow_ps[:, cols], lhsT=infl_t_sb[b][:, j, :], rhs=dec_sb[b][:, dec_cols], start=True, stop=True
+                )
+
+            return [lambda c=c: one(c) for c in range(N_TILE // FLOW_WIDTH)]
 
         def copy_flow(i):
             flow_sb = flow_pool.tile([P, N_TILE], F32)
@@ -197,14 +206,13 @@ def tile_splatinformationflow_pb_kernel(
             flows.append(flow_sb)
 
         def gate_sums(i):
-            m, a = divmod(i, PAIR)
             for h in range(HALVES):
                 gate_ps = psum_gate.tile([P, N_TILE], F32, tag="gate")
                 for g in range(PASSES):
                     nc.tensor.matmul_mx(
                         out=gate_ps[:],
-                        lhsT=x_codes[m][:, a * PASSES + g, :].bitcast(FP8X4),
-                        lhsT_scale=x_scales[m][:, a * PASSES + g, :],
+                        lhsT=x_codes[i][:, g, :].bitcast(FP8X4),
+                        lhsT_scale=x_scales[i][:, g, :],
                         rhs=w_words[:, g, 2 * h * N_TILE : 2 * (h + 1) * N_TILE].bitcast(FP4X4),
                         rhs_scale=w_scales[:, g, half_cols(h)],
                         start=(g == 0),
@@ -237,50 +245,51 @@ def tile_splatinformationflow_pb_kernel(
             )
             nc.sync.dma_start(out=out_view[b, :, j, :], in_=outs[i][:])
 
-        def regroup_pair_on_scalar(m):
-            regroup(m * PAIR, nc.scalar.copy)
-            if m % 2 == 0:
-                regroup(m * PAIR + 1, nc.scalar.copy)
+        def regroup_tile(i):
+            regroup(i, nc.vector.tensor_copy if i % 4 == 3 else nc.scalar.copy)
 
-        transpose_pair(0)
+        def run(calls):
+            for call in calls:
+                call()
+
+        run(token_transposes(0))
         regroup(0, nc.scalar.copy)
+        run(token_transposes(1))
         regroup(1, nc.vector.tensor_copy)
+        quantise(0)
         broadcast_bias()
-        transpose_pair(1)
-        quantise_pair(0)
-        for m in range(N_PAIRS):
-            if m + LOAD_AHEAD < N_PAIRS:
-                load(m + LOAD_AHEAD)
-            ahead = m + 1
-            if ahead < N_PAIRS:
-                regroup_pair_on_scalar(ahead)
-            for a in range(PAIR):
-                i = m * PAIR + a
-                gate_sums(i)
-                if i == 0:
-                    transpose_influences(0)
-                    flow(0, GPSIMD_HALF)
-                    copy_flow(0)
-                if i > 0:
-                    flow(i - 1, VECTOR_HALF)
-                if i + 1 < N_TILES:
-                    flow(i + 1, GPSIMD_HALF)
-                add_bias(i, 0)
-                if a == 1 and ahead < N_PAIRS:
-                    quantise_pair(ahead)
-                add_bias(i, 1)
-                if a == 0 and ahead < N_PAIRS and ahead % 2:
-                    regroup(ahead * PAIR + 1, nc.vector.tensor_copy)
-                if i > 0:
-                    vector_product_and_store(i - 1)
-                sigmoid(i, GPSIMD_HALF)
-                gpsimd_product(i)
-                if i + 1 < N_TILES:
-                    copy_flow(i + 1)
-                sigmoid(i, VECTOR_HALF)
-            if m + 2 < N_PAIRS:
-                if (m + 2) % PAIRS_PER_BATCH == 0:
-                    transpose_influences((m + 2) // PAIRS_PER_BATCH)
-                transpose_pair(m + 2)
-        flow(N_TILES - 1, VECTOR_HALF)
+        quantise(1)
+        run(token_transposes(2))
+        regroup_tile(2)
+        run(token_transposes(3))
+        for i in range(N_TILES):
+            if i % PAIR == 0 and i // PAIR + LOAD_AHEAD < N_PAIRS:
+                load(i // PAIR + LOAD_AHEAD)
+            if i + 3 < N_TILES:
+                regroup_tile(i + 3)
+            gate_sums(i)
+            if i == 0:
+                transpose_influences(0)
+                run(flow_matmuls(0, GPSIMD_HALF))
+                copy_flow(0)
+            f = flow_matmuls(i - 1, VECTOR_HALF) if i > 0 else []
+            t = token_transposes(i + TILES_AHEAD) if i + TILES_AHEAD < N_TILES else []
+            e = flow_matmuls(i + 1, GPSIMD_HALF) if i + 1 < N_TILES else []
+            run(f[:1] + t[:1] + f[1:] + t[1:3] + e[:1] + t[3:])
+            e2 = e[1:]
+            if (i + TILES_AHEAD) % TILES_PER_BATCH == 0 and i + TILES_AHEAD < N_TILES:
+                transpose_influences((i + TILES_AHEAD) // TILES_PER_BATCH)
+            run(e2)
+            add_bias(i, 0)
+            add_bias(i, 1)
+            if i > 0:
+                vector_product_and_store(i - 1)
+            if 2 <= i + 2 < N_TILES:
+                quantise(i + 2)
+            sigmoid(i, GPSIMD_HALF)
+            gpsimd_product(i)
+            if i + 1 < N_TILES:
+                copy_flow(i + 1)
+            sigmoid(i, VECTOR_HALF)
+        run(flow_matmuls(N_TILES - 1, VECTOR_HALF))
         vector_product_and_store(N_TILES - 1)

@@ -24,6 +24,7 @@ N_TILES = BATCHES * TILES_PER_BATCH
 PAIR = 2
 PAIRS_PER_BATCH = TILES_PER_BATCH // PAIR
 N_PAIRS = BATCHES * PAIRS_PER_BATCH
+HEAD_PAIRS = 2
 LOAD_AHEAD = 6
 K_PASS = 4 * P
 PASSES = D // K_PASS
@@ -79,19 +80,19 @@ def tile_splatinformationflow_pb_kernel(
         nc.vector.memset(ones[:], 1.0)
         warm = const.tile([P, 1], F32)
         nc.vector.memset(warm[:], 0.0)
-        nc.scalar.activation(out=warm[:], in_=warm[:], func=SIGMOID)
 
         x_sb = []
         infl_sb = []
         dec_sb = []
 
-        def load_x_pair(m, pieces):
+        def load_x_tile(i):
+            m, a = divmod(i, PAIR)
+            nc.sync.dma_start(out=x_sb[m][:, a, :], in_=x_view[0, :, i, :])
+
+        def load_x_pair(m):
             b, q = divmod(m, PAIRS_PER_BATCH)
             x_pair = x_pool.tile([P, PAIR, D], BF16)
-            width = PAIR // pieces
-            for a in range(0, PAIR, width):
-                j = q * PAIR + a
-                nc.sync.dma_start(out=x_pair[:, a : a + width, :], in_=x_view[b, :, j : j + width, :])
+            nc.sync.dma_start(out=x_pair[:], in_=x_view[b, :, q * PAIR : (q + 1) * PAIR, :])
             x_sb.append(x_pair)
 
         def load_flow_operands(b):
@@ -104,8 +105,10 @@ def tile_splatinformationflow_pb_kernel(
 
         w_words = const.tile([P, PASSES, 2 * D], U8, align_bytes=64)
 
-        def load_gate_weights():
+        def load_gate_words():
             nc.sync.dma_start(out=w_words[:].bitcast(I32), in_=gate_W_words.bitcast(I32).rearrange("g p w -> p g w"))
+
+        def load_gate_scales():
             for r in range(4):
                 nc.sync.dma_start(
                     out=w_scales[:].bitcast(I32)[r:P:32],
@@ -115,14 +118,21 @@ def tile_splatinformationflow_pb_kernel(
         def load(m):
             if m % PAIRS_PER_BATCH == 0 and m > 0:
                 load_flow_operands(m // PAIRS_PER_BATCH)
-            load_x_pair(m, 1)
+            load_x_pair(m)
 
-        load_x_pair(0, PAIR)
-        nc.sync.dma_start(out=bias_rows[0:1, :], in_=gate_b.unsqueeze(0))
-        load_x_pair(1, 1)
-        load_gate_weights()
+        for m in range(HEAD_PAIRS):
+            x_pair = x_pool.tile([P, PAIR, D], BF16)
+            x_sb.append(x_pair)
+        load_x_tile(0)
+        nc.scalar.dma_start(out=bias_rows[0:1, :], in_=gate_b.unsqueeze(0))
+        load_gate_words()
+        load_gate_scales()
+        load_x_tile(1)
+        load_x_tile(2)
         load_flow_operands(0)
-        for m in range(2, LOAD_AHEAD):
+        load_x_tile(3)
+        nc.scalar.activation(out=warm[:], in_=warm[:], func=SIGMOID)
+        for m in range(HEAD_PAIRS, LOAD_AHEAD + 2):
             load(m)
 
         infl_t_sb = []
@@ -243,7 +253,11 @@ def tile_splatinformationflow_pb_kernel(
             nc.vector.tensor_tensor(
                 out=outs[i][:, cols], in0=flow_banks[i, VECTOR_HALF][:], in1=gates[i][:, cols], op=MULT
             )
-            nc.sync.dma_start(out=out_view[b, :, j, :], in_=outs[i][:])
+            if i < N_TILES - 1:
+                nc.sync.dma_start(out=out_view[b, :, j, :], in_=outs[i][:])
+            else:
+                for h in (GPSIMD_HALF, VECTOR_HALF):
+                    nc.sync.dma_start(out=out_view[b, :, j, half_cols(h)], in_=outs[i][:, half_cols(h)])
 
         def regroup_tile(i):
             regroup(i, nc.vector.tensor_copy if i % 4 == 3 else nc.scalar.copy)
@@ -254,25 +268,61 @@ def tile_splatinformationflow_pb_kernel(
 
         run(token_transposes(0))
         regroup(0, nc.scalar.copy)
-        run(token_transposes(1))
-        regroup(1, nc.vector.tensor_copy)
         quantise(0)
         broadcast_bias()
+        run(token_transposes(1))
+        regroup(1, nc.vector.tensor_copy)
+        gate_sums(0)
         quantise(1)
         run(token_transposes(2))
-        regroup_tile(2)
+        regroup(2, nc.scalar.copy)
+        gate_sums(1)
+        add_bias(0, 0)
+        sigmoid(0, GPSIMD_HALF)
+        add_bias(0, 1)
+        sigmoid(0, VECTOR_HALF)
+        transpose_influences(0)
+        quantise(2)
+        add_bias(1, 0)
+        sigmoid(1, GPSIMD_HALF)
         run(token_transposes(3))
-        for i in range(N_TILES):
+        gate_sums(2)
+        add_bias(1, 1)
+        sigmoid(1, VECTOR_HALF)
+        regroup(3, nc.vector.tensor_copy)
+        run(flow_matmuls(0, GPSIMD_HALF))
+        copy_flow(0)
+        gpsimd_product(0)
+        run(token_transposes(4))
+        add_bias(2, 0)
+        run(flow_matmuls(0, VECTOR_HALF))
+        regroup(4, nc.scalar.copy)
+        add_bias(2, 1)
+        sigmoid(2, GPSIMD_HALF)
+        quantise(3)
+        vector_product_and_store(0)
+        run(flow_matmuls(1, GPSIMD_HALF))
+        copy_flow(1)
+        gpsimd_product(1)
+        run(token_transposes(5))
+        run(flow_matmuls(1, VECTOR_HALF))
+        sigmoid(2, VECTOR_HALF)
+        vector_product_and_store(1)
+        quantise(4)
+        run(flow_matmuls(2, GPSIMD_HALF))
+        copy_flow(2)
+        gpsimd_product(2)
+        regroup(5, nc.scalar.copy)
+        run(token_transposes(6))
+        run(flow_matmuls(3, GPSIMD_HALF))
+        copy_flow(3)
+        for i in range(3, N_TILES):
             if i % PAIR == 0 and i // PAIR + LOAD_AHEAD < N_PAIRS:
                 load(i // PAIR + LOAD_AHEAD)
             if i + 3 < N_TILES:
                 regroup_tile(i + 3)
             gate_sums(i)
-            if i == 0:
-                transpose_influences(0)
-                run(flow_matmuls(0, GPSIMD_HALF))
-                copy_flow(0)
-            f = flow_matmuls(i - 1, VECTOR_HALF) if i > 0 else []
+            f = flow_matmuls(i - 1, VECTOR_HALF)
             t = token_transposes(i + TILES_AHEAD) if i + TILES_AHEAD < N_TILES else []
             e = flow_matmuls(i + 1, GPSIMD_HALF) if i + 1 < N_TILES else []
             run(f[:1] + t[:1] + f[1:] + t[1:3] + e[:1] + t[3:])
@@ -282,9 +332,8 @@ def tile_splatinformationflow_pb_kernel(
             run(e2)
             add_bias(i, 0)
             add_bias(i, 1)
-            if i > 0:
-                vector_product_and_store(i - 1)
-            if 2 <= i + 2 < N_TILES:
+            vector_product_and_store(i - 1)
+            if i + 2 < N_TILES:
                 quantise(i + 2)
             sigmoid(i, GPSIMD_HALF)
             gpsimd_product(i)

@@ -29,7 +29,7 @@ LOAD_AHEAD = 6
 K_PASS = 4 * P
 PASSES = D // K_PASS
 WORDS_PER_PASS = K_PASS // 2
-FLOW_WIDTH = 256
+FLOW_WIDTH = 512
 TILES_AHEAD = 4
 N_TILE = 512
 HALVES = D // N_TILE
@@ -69,7 +69,7 @@ def tile_splatinformationflow_pb_kernel(
         out_view = out.rearrange("b (p j) d -> b p j d", j=TILES_PER_BATCH)
 
         bias_rows = const.tile([P, D], BF16)
-        nc.vector.memset(bias_rows[:], 0.0)
+        nc.vector.memset(bias_rows[:].bitcast(I32), 0)
         ident_f32 = const.tile([P, P], F32)
         make_identity(nc, ident_f32[:])
         ident_bf16 = const.tile([P, P], BF16)
@@ -125,9 +125,9 @@ def tile_splatinformationflow_pb_kernel(
             x_sb.append(x_pair)
         load_x_tile(0)
         nc.scalar.dma_start(out=bias_rows[0:1, :], in_=gate_b.unsqueeze(0))
+        load_x_tile(1)
         load_gate_words()
         load_gate_scales()
-        load_x_tile(1)
         load_x_tile(2)
         load_flow_operands(0)
         load_x_tile(3)
@@ -325,8 +325,9 @@ def tile_splatinformationflow_pb_kernel(
             f = flow_matmuls(i - 1, VECTOR_HALF)
             t = token_transposes(i + TILES_AHEAD) if i + TILES_AHEAD < N_TILES else []
             e = flow_matmuls(i + 1, GPSIMD_HALF) if i + 1 < N_TILES else []
-            run(f[:1] + t[:1] + f[1:] + t[1:3] + e[:1] + t[3:])
-            e2 = e[1:]
+            run(f)
+            run(t)
+            e2 = e
             if (i + TILES_AHEAD) % TILES_PER_BATCH == 0 and i + TILES_AHEAD < N_TILES:
                 transpose_influences((i + TILES_AHEAD) // TILES_PER_BATCH)
             run(e2)

@@ -29,6 +29,8 @@ LOAD_AHEAD = 6
 K_PASS = 4 * P
 PASSES = D // K_PASS
 WORDS_PER_PASS = K_PASS // 2
+WARM_UPS = 4
+TAIL_WIDTH = 256
 FLOW_WIDTH = 512
 TILES_AHEAD = 4
 N_TILE = 512
@@ -68,6 +70,8 @@ def tile_splatinformationflow_pb_kernel(
         infl_view = splat_influences.rearrange("b (p j) s -> b p j s", j=TILES_PER_BATCH)
         out_view = out.rearrange("b (p j) d -> b p j d", j=TILES_PER_BATCH)
 
+        zeros = const.tile([P, N_TILE], BF16)
+        nc.vector.memset(zeros[:].bitcast(I32), 0)
         bias_rows = const.tile([P, D], BF16)
         nc.vector.memset(bias_rows[:].bitcast(I32), 0)
         ident_f32 = const.tile([P, P], F32)
@@ -250,17 +254,28 @@ def tile_splatinformationflow_pb_kernel(
         def vector_product_and_store(i):
             b, j = divmod(i, TILES_PER_BATCH)
             cols = half_cols(VECTOR_HALF)
-            nc.vector.tensor_tensor(
-                out=outs[i][:, cols], in0=flow_banks[i, VECTOR_HALF][:], in1=gates[i][:, cols], op=MULT
-            )
             if i < N_TILES - 1:
+                nc.vector.tensor_tensor(
+                    out=outs[i][:, cols], in0=flow_banks[i, VECTOR_HALF][:], in1=gates[i][:, cols], op=MULT
+                )
                 nc.sync.dma_start(out=out_view[b, :, j, :], in_=outs[i][:])
-            else:
-                for h in (GPSIMD_HALF, VECTOR_HALF):
-                    nc.sync.dma_start(out=out_view[b, :, j, half_cols(h)], in_=outs[i][:, half_cols(h)])
+                return
+            for c in range(0, N_TILE, TAIL_WIDTH):
+                bank_cols = slice(c, c + TAIL_WIDTH)
+                out_cols = slice(VECTOR_HALF * N_TILE + c, VECTOR_HALF * N_TILE + c + TAIL_WIDTH)
+                nc.vector.tensor_tensor(
+                    out=outs[i][:, out_cols], in0=flow_banks[i, VECTOR_HALF][:, bank_cols], in1=gates[i][:, out_cols], op=MULT
+                )
+                nc.sync.dma_start(out=out_view[b, :, j, out_cols], in_=outs[i][:, out_cols])
+            cols = half_cols(GPSIMD_HALF)
+            nc.sync.dma_start(out=out_view[b, :, j, cols], in_=outs[i][:, cols])
+
+        idle_ps = psum_flow.tile([P, N_TILE], F32, tag="flow")
+        for r in range(WARM_UPS):
+            nc.tensor.matmul(idle_ps[:], lhsT=zeros[:, 0:P], rhs=zeros[:], start=True, stop=True)
 
         def regroup_tile(i):
-            regroup(i, nc.vector.tensor_copy if i % 4 == 3 else nc.scalar.copy)
+            regroup(i, nc.vector.tensor_copy if i % 4 == 0 else nc.scalar.copy)
 
         def run(calls):
             for call in calls:
@@ -269,8 +284,8 @@ def tile_splatinformationflow_pb_kernel(
         run(token_transposes(0))
         regroup(0, nc.scalar.copy)
         quantise(0)
-        broadcast_bias()
         run(token_transposes(1))
+        broadcast_bias()
         regroup(1, nc.vector.tensor_copy)
         gate_sums(0)
         quantise(1)

@@ -214,9 +214,13 @@ def tile_splatinformationflow_pb_kernel(
 
             return [lambda c=c: one(c) for c in range(N_TILE // FLOW_WIDTH)]
 
+        def gpsimd_width(i):
+            return N_TILE if i < N_TILES - 1 else TAIL_WIDTH
+
         def copy_flow(i):
+            width = gpsimd_width(i)
             flow_sb = flow_pool.tile([P, N_TILE], F32)
-            nc.scalar.copy(out=flow_sb[:], in_=flow_banks[i, GPSIMD_HALF][:])
+            nc.scalar.copy(out=flow_sb[:, 0:width], in_=flow_banks[i, GPSIMD_HALF][:, 0:width])
             flows.append(flow_sb)
 
         def gate_sums(i):
@@ -247,9 +251,12 @@ def tile_splatinformationflow_pb_kernel(
 
         def gpsimd_product(i):
             out_sb = out_pool.tile([P, D], F32)
-            cols = half_cols(GPSIMD_HALF)
-            nc.gpsimd.tensor_tensor(out=out_sb[:, cols], in0=flows[i][:], in1=gates[i][:, cols], op=MULT)
+            cols = slice(0, gpsimd_width(i))
+            nc.gpsimd.tensor_tensor(out=out_sb[:, cols], in0=flows[i][:, cols], in1=gates[i][:, cols], op=MULT)
             outs.append(out_sb)
+            if i == N_TILES - 2:
+                b, j = divmod(i, TILES_PER_BATCH)
+                nc.sync.dma_start(out=out_view[b, :, j, cols], in_=out_sb[:, cols])
 
         def vector_product_and_store(i):
             b, j = divmod(i, TILES_PER_BATCH)
@@ -258,17 +265,22 @@ def tile_splatinformationflow_pb_kernel(
                 nc.vector.tensor_tensor(
                     out=outs[i][:, cols], in0=flow_banks[i, VECTOR_HALF][:], in1=gates[i][:, cols], op=MULT
                 )
-                nc.sync.dma_start(out=out_view[b, :, j, :], in_=outs[i][:])
+                if i < N_TILES - 2:
+                    nc.sync.dma_start(out=out_view[b, :, j, :], in_=outs[i][:])
+                else:
+                    nc.sync.dma_start(out=out_view[b, :, j, cols], in_=outs[i][:, cols])
                 return
-            for c in range(0, N_TILE, TAIL_WIDTH):
-                bank_cols = slice(c, c + TAIL_WIDTH)
-                out_cols = slice(VECTOR_HALF * N_TILE + c, VECTOR_HALF * N_TILE + c + TAIL_WIDTH)
-                nc.vector.tensor_tensor(
-                    out=outs[i][:, out_cols], in0=flow_banks[i, VECTOR_HALF][:, bank_cols], in1=gates[i][:, out_cols], op=MULT
-                )
-                nc.sync.dma_start(out=out_view[b, :, j, out_cols], in_=outs[i][:, out_cols])
-            cols = half_cols(GPSIMD_HALF)
-            nc.sync.dma_start(out=out_view[b, :, j, cols], in_=outs[i][:, cols])
+            for c in range(0, D, TAIL_WIDTH):
+                h, first = divmod(c, N_TILE)
+                cols = slice(c, c + TAIL_WIDTH)
+                if c >= gpsimd_width(i):
+                    nc.vector.tensor_tensor(
+                        out=outs[i][:, cols],
+                        in0=flow_banks[i, h][:, first : first + TAIL_WIDTH],
+                        in1=gates[i][:, cols],
+                        op=MULT,
+                    )
+                nc.sync.dma_start(out=out_view[b, :, j, cols], in_=outs[i][:, cols])
 
         idle_ps = psum_flow.tile([P, N_TILE], F32, tag="flow")
         for r in range(WARM_UPS):
@@ -348,9 +360,9 @@ def tile_splatinformationflow_pb_kernel(
             run(e2)
             add_bias(i, 0)
             add_bias(i, 1)
-            vector_product_and_store(i - 1)
             if i + 2 < N_TILES:
                 quantise(i + 2)
+            vector_product_and_store(i - 1)
             sigmoid(i, GPSIMD_HALF)
             gpsimd_product(i)
             if i + 1 < N_TILES:

@@ -25,12 +25,13 @@ PAIR = 2
 PAIRS_PER_BATCH = TILES_PER_BATCH // PAIR
 N_PAIRS = BATCHES * PAIRS_PER_BATCH
 HEAD_PAIRS = 2
-LOAD_AHEAD = 6
+LOAD_AHEAD = 5
 K_PASS = 4 * P
 PASSES = D // K_PASS
 WORDS_PER_PASS = K_PASS // 2
 WARM_UPS = 4
 TAIL_WIDTH = 256
+GPSIMD_WIDTH = 256
 FLOW_WIDTH = 512
 TILES_AHEAD = 4
 N_TILE = 512
@@ -60,7 +61,7 @@ def tile_splatinformationflow_pb_kernel(
         mx_pool = ctx.enter_context(tc.tile_pool(name="mx", bufs=6))
         gate_pool = ctx.enter_context(tc.tile_pool(name="gate", bufs=5))
         flow_pool = ctx.enter_context(tc.tile_pool(name="flow", bufs=4))
-        out_pool = ctx.enter_context(tc.tile_pool(name="outs", bufs=10))
+        out_pool = ctx.enter_context(tc.tile_pool(name="outs", bufs=28))
         psum_t = ctx.enter_context(tc.psum_pool(name="psum_t", bufs=TRANSPOSE_BANKS))
         psum_gate = ctx.enter_context(tc.psum_pool(name="psum_gate", bufs=GATE_BANKS))
         psum_flow = ctx.enter_context(tc.psum_pool(name="psum_flow", bufs=FLOW_BANKS))
@@ -251,8 +252,10 @@ def tile_splatinformationflow_pb_kernel(
 
         def gpsimd_product(i):
             out_sb = out_pool.tile([P, D], F32)
+            for c in range(0, gpsimd_width(i), GPSIMD_WIDTH):
+                part = slice(c, c + GPSIMD_WIDTH)
+                nc.gpsimd.tensor_tensor(out=out_sb[:, part], in0=flows[i][:, part], in1=gates[i][:, part], op=MULT)
             cols = slice(0, gpsimd_width(i))
-            nc.gpsimd.tensor_tensor(out=out_sb[:, cols], in0=flows[i][:, cols], in1=gates[i][:, cols], op=MULT)
             outs.append(out_sb)
             if i == N_TILES - 2:
                 b, j = divmod(i, TILES_PER_BATCH)
@@ -360,9 +363,9 @@ def tile_splatinformationflow_pb_kernel(
             run(e2)
             add_bias(i, 0)
             add_bias(i, 1)
+            vector_product_and_store(i - 1)
             if i + 2 < N_TILES:
                 quantise(i + 2)
-            vector_product_and_store(i - 1)
             sigmoid(i, GPSIMD_HALF)
             gpsimd_product(i)
             if i + 1 < N_TILES:

@@ -32,7 +32,7 @@ WORDS_PER_PASS = K_PASS // 2
 WARM_UPS = 4
 TAIL_WIDTH = 256
 GPSIMD_WIDTH = 256
-FLOW_WIDTH = 512
+FLOW_WIDTH = 256
 TILES_AHEAD = 4
 N_TILE = 512
 HALVES = D // N_TILE
@@ -355,12 +355,10 @@ def tile_splatinformationflow_pb_kernel(
             f = flow_matmuls(i - 1, VECTOR_HALF)
             t = token_transposes(i + TILES_AHEAD) if i + TILES_AHEAD < N_TILES else []
             e = flow_matmuls(i + 1, GPSIMD_HALF) if i + 1 < N_TILES else []
-            run(f)
-            run(t)
-            e2 = e
+            run(f[:1] + t[:1] + f[1:] + t[1:2])
             if (i + TILES_AHEAD) % TILES_PER_BATCH == 0 and i + TILES_AHEAD < N_TILES:
                 transpose_influences((i + TILES_AHEAD) // TILES_PER_BATCH)
-            run(e2)
+            run(e[:1] + t[2:] + e[1:])
             add_bias(i, 0)
             add_bias(i, 1)
             vector_product_and_store(i - 1)

from contextlib import ExitStack

import concourse.mybir as mybir
from concourse.masks import make_identity

F32 = mybir.dt.float32
BF16 = mybir.dt.bfloat16
I32 = mybir.dt.int32
U32 = mybir.dt.uint32
U8 = mybir.dt.uint8
FP8X4 = mybir.dt.float8_e4m3fn_x4
FP4X4 = mybir.dt.float4_e2m1fn_x4
ADD = mybir.AluOpType.add
MULT = mybir.AluOpType.mult
SIGMOID = mybir.ActivationFunctionType.Sigmoid

P = 128
BATCHES = 4
TOKENS = 1024
D = 1024
SPLATS = 128
TILES_PER_BATCH = TOKENS // P
N_TILES = BATCHES * TILES_PER_BATCH
PAIR = 2
PAIRS_PER_BATCH = TILES_PER_BATCH // PAIR
N_PAIRS = BATCHES * PAIRS_PER_BATCH
HEAD_PAIRS = 2
LOAD_AHEAD = 5
K_PASS = 4 * P
PASSES = D // K_PASS
WORDS_PER_PASS = K_PASS // 2
WARM_UPS = 4
TAIL_WIDTH = 256
GPSIMD_WIDTH = 256
FLOW_WIDTH = 256
TILES_AHEAD = 4
N_TILE = 512
HALVES = D // N_TILE
GPSIMD_HALF = 0
VECTOR_HALF = 1
TRANSPOSE_BANKS = 2
GATE_BANKS = 3
FLOW_BANKS = 3

FLOPS = 2 * BATCHES * TOKENS * D * D + 2 * BATCHES * TOKENS * SPLATS * D


def half_cols(h):
    return slice(h * N_TILE, (h + 1) * N_TILE)


def tile_splatinformationflow_pb_kernel(
    tc, token_embeddings, splat_influences, decoded, gate_W_words, gate_W_scales, gate_b, out
):
    nc = tc.nc
    with ExitStack() as ctx:
        const = ctx.enter_context(tc.tile_pool(name="const", bufs=1))
        x_pool = ctx.enter_context(tc.tile_pool(name="x", bufs=LOAD_AHEAD + 2))
        batch_pool = ctx.enter_context(tc.tile_pool(name="batch", bufs=BATCHES))
        grouped_pool = ctx.enter_context(tc.tile_pool(name="grouped", bufs=4))
        mx_pool = ctx.enter_context(tc.tile_pool(name="mx", bufs=6))
        gate_pool = ctx.enter_context(tc.tile_pool(name="gate", bufs=5))
        flow_pool = ctx.enter_context(tc.tile_pool(name="flow", bufs=4))
        out_pool = ctx.enter_context(tc.tile_pool(name="outs", bufs=28))
        psum_t = ctx.enter_context(tc.psum_pool(name="psum_t", bufs=TRANSPOSE_BANKS))
        psum_gate = ctx.enter_context(tc.psum_pool(name="psum_gate", bufs=GATE_BANKS))
        psum_flow = ctx.enter_context(tc.psum_pool(name="psum_flow", bufs=FLOW_BANKS))
        ctx.enter_context(tc.manual_schedule())

        x_view = token_embeddings.rearrange("b (p j) k -> b p j k", j=TILES_PER_BATCH)
        infl_view = splat_influences.rearrange("b (p j) s -> b p j s", j=TILES_PER_BATCH)
        out_view = out.rearrange("b (p j) d -> b p j d", j=TILES_PER_BATCH)

        zeros = const.tile([P, N_TILE], BF16)
        nc.vector.memset(zeros[:].bitcast(I32), 0)
        bias_rows = const.tile([P, D], BF16)
        nc.vector.memset(bias_rows[:].bitcast(I32), 0)
        ident_f32 = const.tile([P, P], F32)
        make_identity(nc, ident_f32[:])
        ident_bf16 = const.tile([P, P], BF16)
        make_identity(nc, ident_bf16[:])
        w_scales = const.tile([P, PASSES, D], U8, align_bytes=64)
        nc.vector.memset(w_scales[:].rearrange("p g n -> p (g n)").bitcast(I32), 0)
        ones = const.tile([P, P], BF16)
        nc.vector.memset(ones[:], 1.0)
        warm = const.tile([P, 1], F32)
        nc.vector.memset(warm[:], 0.0)

        x_sb = []
        infl_sb = []
        dec_sb = []

        def load_x_tile(i):
            m, a = divmod(i, PAIR)
            nc.sync.dma_start(out=x_sb[m][:, a, :], in_=x_view[0, :, i, :])

        def load_x_pair(m):
            b, q = divmod(m, PAIRS_PER_BATCH)
            x_pair = x_pool.tile([P, PAIR, D], BF16)
            nc.sync.dma_start(out=x_pair[:], in_=x_view[b, :, q * PAIR : (q + 1) * PAIR, :])
            x_sb.append(x_pair)

        def load_flow_operands(b):
            infl = batch_pool.tile([P, TILES_PER_BATCH, SPLATS], BF16)
            nc.sync.dma_start(out=infl[:], in_=infl_view[b])
            infl_sb.append(infl)
            dec = batch_pool.tile([SPLATS, D], BF16)
            nc.sync.dma_start(out=dec[:], in_=decoded[b])
            dec_sb.append(dec)

        w_words = const.tile([P, PASSES, 2 * D], U8, align_bytes=64)

        def load_gate_words():
            nc.sync.dma_start(out=w_words[:].bitcast(I32), in_=gate_W_words.bitcast(I32).rearrange("g p w -> p g w"))

        def load_gate_scales():
            for r in range(4):
                nc.sync.dma_start(
                    out=w_scales[:].bitcast(I32)[r:P:32],
                    in_=gate_W_scales.bitcast(I32)[:, r:16:4, :].rearrange("g q n -> q g n"),
                )

        def load(m):
            if m % PAIRS_PER_BATCH == 0 and m > 0:
                load_flow_operands(m // PAIRS_PER_BATCH)
            load_x_pair(m)

        for m in range(HEAD_PAIRS):
            x_pair = x_pool.tile([P, PAIR, D], BF16)
            x_sb.append(x_pair)
        load_x_tile(0)
        nc.scalar.dma_start(out=bias_rows[0:1, :], in_=gate_b.unsqueeze(0))
        load_x_tile(1)
        load_gate_words()
        load_gate_scales()
        load_x_tile(2)
        load_flow_operands(0)
        load_x_tile(3)
        nc.scalar.activation(out=warm[:], in_=warm[:], func=SIGMOID)
        for m in range(HEAD_PAIRS, LOAD_AHEAD + 2):
            load(m)

        infl_t_sb = []
        xt_banks = []
        grouped_sb = []
        x_codes = []
        x_scales = []
        gate_banks = {}
        gates = []
        flow_banks = {}
        flows = []
        outs = []

        bias_f32 = const.tile([P, D], F32)

        def broadcast_bias():
            for h in range(HALVES):
                bias_ps = psum_flow.tile([P, N_TILE], F32, tag="flow")
                nc.tensor.matmul(bias_ps[:], lhsT=ones[:], rhs=bias_rows[:, half_cols(h)], start=True, stop=True)
                nc.scalar.copy(out=bias_f32[:, half_cols(h)], in_=bias_ps[:])

        def transpose_influences(b):
            it_ps = psum_flow.tile([SPLATS, TILES_PER_BATCH, P], BF16, tag="flow")
            for j in range(TILES_PER_BATCH):
                nc.tensor.transpose(it_ps[:, j, :], infl_sb[b][:, j, :], ident_bf16[:])
            infl_t = batch_pool.tile([SPLATS, TILES_PER_BATCH, P], BF16)
            nc.scalar.copy(out=infl_t[:], in_=it_ps[:])
            infl_t_sb.append(infl_t)

        def token_transposes(i):
            m, a = divmod(i, PAIR)
            x_words = x_sb[m][:].bitcast(F32)
            xt_ps = psum_t.tile([P, PASSES * 2, P], F32, tag="xt")
            xt_banks.append(xt_ps)

            def one(g, u):
                nc.tensor.transpose(
                    xt_ps[:, 2 * g + u, :],
                    x_words[:, a, g * WORDS_PER_PASS + u : (g + 1) * WORDS_PER_PASS : 2],
                    ident_f32[:],
                )

            return [lambda g=g, u=u: one(g, u) for g in range(PASSES) for u in range(2)]

        def regroup(i, copy):
            grouped = grouped_pool.tile([P, D], BF16, align_bytes=64)
            grouped_sb.append(grouped)
            copy(
                out=grouped[:].bitcast(F32).rearrange("p (g r u) -> p g r u", g=PASSES, u=2),
                in_=xt_banks[i][:].rearrange("p (g u) r -> p g r u", u=2),
            )

        def quantise(i):
            codes = mx_pool.tile([P, PASSES, P], U32, align_bytes=64)
            scales = mx_pool.tile([P, PASSES, P], U8, align_bytes=64)
            nc.vector.quantize_mx(
                out=codes[:].rearrange("p g r -> p (g r)").bitcast(FP8X4),
                scales=scales[:].rearrange("p g r -> p (g r)"),
                in_=grouped_sb[i][:],
            )
            x_codes.append(codes)
            x_scales.append(scales)

        def flow_matmuls(i, h):
            b, j = divmod(i, TILES_PER_BATCH)
            flow_ps = psum_flow.tile([P, N_TILE], F32, tag="flow")
            flow_banks[i, h] = flow_ps

            def one(c):
                cols = slice(c * FLOW_WIDTH, (c + 1) * FLOW_WIDTH)
                dec_cols = slice(h * N_TILE + c * FLOW_WIDTH, h * N_TILE + (c + 1) * FLOW_WIDTH)
                nc.tensor.matmul(
                    flow_ps[:, cols], lhsT=infl_t_sb[b][:, j, :], rhs=dec_sb[b][:, dec_cols], start=True, stop=True
                )

            return [lambda c=c: one(c) for c in range(N_TILE // FLOW_WIDTH)]

        def gpsimd_width(i):
            return N_TILE if i < N_TILES - 1 else TAIL_WIDTH

        def copy_flow(i):
            width = gpsimd_width(i)
            flow_sb = flow_pool.tile([P, N_TILE], F32)
            nc.scalar.copy(out=flow_sb[:, 0:width], in_=flow_banks[i, GPSIMD_HALF][:, 0:width])
            flows.append(flow_sb)

        def gate_sums(i):
            for h in range(HALVES):
                gate_ps = psum_gate.tile([P, N_TILE], F32, tag="gate")
                for g in range(PASSES):
                    nc.tensor.matmul_mx(
                        out=gate_ps[:],
                        lhsT=x_codes[i][:, g, :].bitcast(FP8X4),
                        lhsT_scale=x_scales[i][:, g, :],
                        rhs=w_words[:, g, 2 * h * N_TILE : 2 * (h + 1) * N_TILE].bitcast(FP4X4),
                        rhs_scale=w_scales[:, g, half_cols(h)],
                        start=(g == 0),
                        stop=(g == PASSES - 1),
                    )
                gate_banks[i, h] = gate_ps

        def add_bias(i, h):
            if h == 0:
                gate_sb = gate_pool.tile([P, D], F32)
                gates.append(gate_sb)
            nc.vector.tensor_tensor(
                out=gates[i][:, half_cols(h)], in0=gate_banks[i, h][:], in1=bias_f32[:, half_cols(h)], op=ADD
            )

        def sigmoid(i, h):
            nc.scalar.activation(out=gates[i][:, half_cols(h)], in_=gates[i][:, half_cols(h)], func=SIGMOID)

        def gpsimd_product(i):
            out_sb = out_pool.tile([P, D], F32)
            for c in range(0, gpsimd_width(i), GPSIMD_WIDTH):
                part = slice(c, c + GPSIMD_WIDTH)
                nc.gpsimd.tensor_tensor(out=out_sb[:, part], in0=flows[i][:, part], in1=gates[i][:, part], op=MULT)
            cols = slice(0, gpsimd_width(i))
            outs.append(out_sb)
            if i == N_TILES - 2:
                b, j = divmod(i, TILES_PER_BATCH)
                nc.sync.dma_start(out=out_view[b, :, j, cols], in_=out_sb[:, cols])

        def vector_product_and_store(i):
            b, j = divmod(i, TILES_PER_BATCH)
            cols = half_cols(VECTOR_HALF)
            if i < N_TILES - 1:
                nc.vector.tensor_tensor(
                    out=outs[i][:, cols], in0=flow_banks[i, VECTOR_HALF][:], in1=gates[i][:, cols], op=MULT
                )
                if i < N_TILES - 2:
                    nc.sync.dma_start(out=out_view[b, :, j, :], in_=outs[i][:])
                else:
                    nc.sync.dma_start(out=out_view[b, :, j, cols], in_=outs[i][:, cols])
                return
            for c in range(0, D, TAIL_WIDTH):
                h, first = divmod(c, N_TILE)
                cols = slice(c, c + TAIL_WIDTH)
                if c >= gpsimd_width(i):
                    nc.vector.tensor_tensor(
                        out=outs[i][:, cols],
                        in0=flow_banks[i, h][:, first : first + TAIL_WIDTH],
                        in1=gates[i][:, cols],
                        op=MULT,
                    )
                nc.sync.dma_start(out=out_view[b, :, j, cols], in_=outs[i][:, cols])

        idle_ps = psum_flow.tile([P, N_TILE], F32, tag="flow")
        for r in range(WARM_UPS):
            nc.tensor.matmul(idle_ps[:], lhsT=zeros[:, 0:P], rhs=zeros[:], start=True, stop=True)

        def regroup_tile(i):
            regroup(i, nc.vector.tensor_copy if i % 4 == 0 else nc.scalar.copy)

        def run(calls):
            for call in calls:
                call()

        run(token_transposes(0))
        regroup(0, nc.scalar.copy)
        quantise(0)
        run(token_transposes(1))
        broadcast_bias()
        regroup(1, nc.vector.tensor_copy)
        gate_sums(0)
        quantise(1)
        run(token_transposes(2))
        regroup(2, nc.scalar.copy)
        gate_sums(1)
        add_bias(0, 0)
        sigmoid(0, GPSIMD_HALF)
        add_bias(0, 1)
        sigmoid(0, VECTOR_HALF)
        transpose_influences(0)
        quantise(2)
        add_bias(1, 0)
        sigmoid(1, GPSIMD_HALF)
        run(token_transposes(3))
        gate_sums(2)
        add_bias(1, 1)
        sigmoid(1, VECTOR_HALF)
        regroup(3, nc.vector.tensor_copy)
        run(flow_matmuls(0, GPSIMD_HALF))
        copy_flow(0)
        gpsimd_product(0)
        run(token_transposes(4))
        add_bias(2, 0)
        run(flow_matmuls(0, VECTOR_HALF))
        regroup(4, nc.scalar.copy)
        add_bias(2, 1)
        sigmoid(2, GPSIMD_HALF)
        quantise(3)
        vector_product_and_store(0)
        run(flow_matmuls(1, GPSIMD_HALF))
        copy_flow(1)
        gpsimd_product(1)
        run(token_transposes(5))
        run(flow_matmuls(1, VECTOR_HALF))
        sigmoid(2, VECTOR_HALF)
        vector_product_and_store(1)
        quantise(4)
        run(flow_matmuls(2, GPSIMD_HALF))
        copy_flow(2)
        gpsimd_product(2)
        regroup(5, nc.scalar.copy)
        run(token_transposes(6))
        run(flow_matmuls(3, GPSIMD_HALF))
        copy_flow(3)
        for i in range(3, N_TILES):
            if i % PAIR == 0 and i // PAIR + LOAD_AHEAD < N_PAIRS:
                load(i // PAIR + LOAD_AHEAD)
            if i + 3 < N_TILES:
                regroup_tile(i + 3)
            gate_sums(i)
            f = flow_matmuls(i - 1, VECTOR_HALF)
            t = token_transposes(i + TILES_AHEAD) if i + TILES_AHEAD < N_TILES else []
            e = flow_matmuls(i + 1, GPSIMD_HALF) if i + 1 < N_TILES else []
            run(f[:1] + t[:1] + f[1:] + t[1:2])
            if (i + TILES_AHEAD) % TILES_PER_BATCH == 0 and i + TILES_AHEAD < N_TILES:
                transpose_influences((i + TILES_AHEAD) // TILES_PER_BATCH)
            run(e[:1] + t[2:] + e[1:])
            add_bias(i, 0)
            add_bias(i, 1)
            vector_product_and_store(i - 1)
            if i + 2 < N_TILES:
                quantise(i + 2)
            sigmoid(i, GPSIMD_HALF)
            gpsimd_product(i)
            if i + 1 < N_TILES:
                copy_flow(i + 1)
            sigmoid(i, VECTOR_HALF)
        run(flow_matmuls(N_TILES - 1, VECTOR_HALF))
        vector_product_and_store(N_TILES - 1)
